import numpy as np
import ml_dtypes


def mxq(x, axis, fmt="e4m3"):
    dtype, down = {"e4m3": (ml_dtypes.float8_e4m3fn, 7), "e5m2": (ml_dtypes.float8_e5m2, 14)}[fmt]
    v = np.moveaxis(np.asarray(x, np.float32).astype(ml_dtypes.bfloat16).astype(np.float64), axis, -1)
    blocks = v.reshape(v.shape[:-1] + (-1, 32))
    amax = np.abs(blocks).max(-1, keepdims=True)
    byte = np.maximum(np.where(amax > 0, np.frexp(amax)[1] - 1 + 127, 0) - down, 1)
    scale = np.exp2(byte - 127.0)
    codes = (blocks / scale).astype(np.float32).astype(dtype).astype(np.float64)
    return np.moveaxis((codes * scale).reshape(v.shape), -1, axis)


WIDE = False


def mx_kscale(k):
    if not WIDE:
        return np.ones(k)
    levels = np.array([10, -10, 5, -5, 0])
    a = np.random.permutation(np.resize(levels, k // 512 * 4)).reshape(k // 512, 4)
    idx = np.arange(k)
    return np.exp2(a[idx // 512, idx % 128 // 32])


BF16 = ml_dtypes.bfloat16


def bf(x):
    return np.asarray(x, np.float32).astype(BF16)


def f64(x):
    return np.asarray(x).astype(np.float64)


B, N, D, F, C, L = 1024, 4096, 1024, 1024, 128, 28
EPS = 1e-12
P = 3


def unit_rows(m, k):
    x = np.random.standard_normal((m, k))
    return x / np.sqrt(np.sum(x * x, axis=1, keepdims=True))


def setup_inputs():
    s = mx_kscale(F)
    return {"f_unit": bf(unit_rows(B, F) * s),
            "exf_unit": bf(unit_rows(N, F) / s),
            "ex_class_reps": bf((np.random.uniform(size=(N, C)) * 2.0 - 1.0) * 0.15 * np.sqrt(N)),
            "class_reps": bf((np.random.uniform(size=(L, C)) * 2.0 - 1.0) * 0.4)}


def reference(f_unit, exf_unit, ex_class_reps, class_reps):
    s = mxq(f64(f_unit), 1, "e4m3") @ mxq(f64(exf_unit), 1, "e4m3").T
    a = np.sign(s) * np.abs(s) ** P
    a = a / np.maximum(np.sum(np.abs(a), axis=1, keepdims=True), EPS)
    echo = mxq(a, 1, "e4m3") @ mxq(f64(ex_class_reps), 0, "e4m3")
    diff = echo[:, None, :] - f64(class_reps)[None, :, :]
    return -np.sqrt(np.sum(diff * diff, axis=-1))

@@ -1,0 +1,235 @@
+from contextlib import ExitStack
+
+import concourse.mybir as mybir
+from concourse.masks import make_identity
+
+F32 = mybir.dt.float32
+BF16 = mybir.dt.bfloat16
+U32 = mybir.dt.uint32
+U8 = mybir.dt.uint8
+FP8X4 = mybir.dt.float8_e4m3fn_x4
+ACT = mybir.ActivationFunctionType
+ALU = mybir.AluOpType
+AXIS = mybir.AxisListType
+
+P = 128
+PACK = 4
+K_PASS = P * PACK
+
+B, N, F, C, L = 1024, 4096, 1024, 128, 28
+EPS = 1e-12
+
+B_TILES = B // P
+N_CHUNKS = N // K_PASS
+F_PASSES = F // K_PASS
+ROW_TILES = K_PASS // P
+L_PAD = 32
+
+UNITS = B_TILES * N_CHUNKS
+RUN = 2
+LAG = N_CHUNKS + RUN
+AHEAD = 3
+
+FLOPS = 2 * B * N * F + 2 * B * N * C
+
+
+def tile_minerva_old_pb_kernel(tc, f_unit, exf_unit, ex_class_reps, class_reps, out):
+    nc = tc.nc
+    with ExitStack() as stack:
+        consts = stack.enter_context(tc.tile_pool(name="consts", bufs=1))
+        keep = stack.enter_context(tc.tile_pool(name="keep", bufs=1))
+        raw_pool = stack.enter_context(tc.tile_pool(name="raw", bufs=AHEAD + 1))
+        stage = stack.enter_context(tc.tile_pool(name="stage", bufs=2))
+        a_pool = stack.enter_context(tc.tile_pool(name="a", bufs=3))
+        work = stack.enter_context(tc.tile_pool(name="work", bufs=3))
+        small = stack.enter_context(tc.tile_pool(name="small", bufs=2))
+        psum_s = stack.enter_context(tc.psum_pool(name="psum_s", bufs=3))
+        psum_t = stack.enter_context(tc.psum_pool(name="psum_t", bufs=3))
+        psum_e = stack.enter_context(tc.psum_pool(name="psum_e", bufs=1))
+        psum_m = stack.enter_context(tc.psum_pool(name="psum_m", bufs=1))
+
+        ident_f32 = consts.tile([P, P], F32)
+        make_identity(nc, ident_f32[:])
+        ident_bf16 = consts.tile([P, P], BF16)
+        make_identity(nc, ident_bf16[:])
+        ones = consts.tile([P, P], F32)
+        nc.vector.memset(ones[:], 1.0)
+        warm = consts.tile([P, 1], F32)
+        nc.scalar.activation(out=warm[:], in_=ones[:, 0:1], func=ACT.Sqrt)
+
+        f_codes = keep.tile([P, F_PASSES, B], U32, align_bytes=64)
+        f_scales = keep.tile([P, F_PASSES, B], U8, align_bytes=64)
+        x_codes = keep.tile([P, F_PASSES, N], U32, align_bytes=64)
+        x_scales = keep.tile([P, F_PASSES, N], U8, align_bytes=64)
+        e_codes = keep.tile([P, N_CHUNKS * C], U32, align_bytes=64)
+        e_scales = keep.tile([P, N_CHUNKS * C], U8, align_bytes=64)
+        dist_sq = keep.tile([P, B_TILES, L], F32)
+
+        f_rows = f_unit.rearrange("(p j) k -> p j k", j=B_TILES)
+        blocks = [f_rows[:, 0:ROW_TILES, :]]
+        for c in range(N_CHUNKS):
+            blocks.append(exf_unit[c * K_PASS : (c + 1) * K_PASS, :].rearrange("(p t) k -> p t k", t=PACK))
+        blocks.append(f_rows[:, ROW_TILES : 2 * ROW_TILES, :])
+        blocks.append(ex_class_reps.rearrange("(g p t) c -> p g (t c)", p=P, t=PACK))
+        F_BLOCKS = (0, N_CHUNKS + 1)
+        E_BLOCK = N_CHUNKS + 2
+        raw_tiles = {}
+
+        def load_block(i):
+            raw_tiles[i] = raw_pool.tile([P, ROW_TILES * F], BF16, name="raw", tag="raw")
+            nc.sync.dma_start(out=raw_tiles[i][:].rearrange("p (r x) -> p r x", r=blocks[i].shape[1]), in_=blocks[i])
+
+        def take_block(i):
+            if i + AHEAD < len(blocks):
+                load_block(i + AHEAD)
+            return raw_tiles[i]
+
+        def rows_to_mx(raw, codes, scales, cols):
+            words = raw[:].bitcast(F32).rearrange("p (r w) -> p r w", r=ROW_TILES)
+            grouped = stage.tile([P, F_PASSES, K_PASS * PACK], BF16, tag="grouped", align_bytes=64)
+            grouped_words = grouped[:].bitcast(F32).rearrange("p g (r m u) -> p g r m u", r=ROW_TILES, u=2)
+            for r in range(ROW_TILES):
+                planes = psum_t.tile([P, F_PASSES, 2, P], F32, tag="t")
+                for g in range(F_PASSES):
+                    for u in range(2):
+                        first = (2 * g + u) * P
+                        nc.tensor.transpose(planes[:, g, u, :], words[:, r, first : first + P], ident_f32[:])
+                nc.scalar.copy(out=grouped_words[:, :, r, :, :], in_=planes[:].rearrange("p g u m -> p g m u"))
+            for g in range(F_PASSES):
+                nc.vector.quantize_mx(
+                    out=codes[:, g, cols].bitcast(FP8X4), scales=scales[:, g, cols], in_=grouped[:, g, :]
+                )
+
+        for i in range(AHEAD):
+            load_block(i)
+
+        cls_pad = consts.tile([P, C], BF16)
+        nc.vector.memset(cls_pad[:], 0.0)
+        nc.sync.dma_start(out=cls_pad[0:L, :], in_=class_reps)
+        cls_ps = psum_m.tile([P, P], BF16, tag="m")
+        nc.tensor.transpose(cls_ps[:], cls_pad[:], ident_bf16[:])
+        cls_t = consts.tile([P, L_PAD], F32)
+        nc.vector.tensor_copy(out=cls_t[:], in_=cls_ps[:, 0:L_PAD])
+        cls_m2 = consts.tile([P, L_PAD], F32)
+        nc.vector.tensor_scalar(out=cls_m2[:], in0=cls_t[:], scalar1=-2.0, scalar2=None, op0=ALU.mult)
+        cls_sq = consts.tile([P, L_PAD], F32)
+        nc.vector.tensor_tensor(out=cls_sq[:], in0=cls_t[:], in1=cls_t[:], op=ALU.mult)
+
+        rows_to_mx(take_block(F_BLOCKS[0]), f_codes, f_scales, slice(0, K_PASS))
+
+        a_tiles = {}
+        abs_sums = {}
+        inv_rows = {}
+        a_grouped = {}
+
+        def similarities(j, c):
+            if c == 0:
+                a_tiles[j] = a_pool.tile([P, N], F32, name="a_rows", tag="a")
+                abs_sums[j] = small.tile([P, N_CHUNKS], F32, name="abs_sums", tag="abs_sums", bufs=3)
+            probes = slice(j * P, (j + 1) * P)
+            chunk = slice(c * K_PASS, (c + 1) * K_PASS)
+            s_ps = psum_s.tile([P, K_PASS], F32, tag="s")
+            for g in range(F_PASSES):
+                nc.tensor.matmul_mx(
+                    out=s_ps[:],
+                    lhsT=f_codes[:, g, probes].bitcast(FP8X4),
+                    lhsT_scale=f_scales[:, g, probes],
+                    rhs=x_codes[:, g, chunk].bitcast(FP8X4),
+                    rhs_scale=x_scales[:, g, chunk],
+                    start=(g == 0),
+                    stop=(g == F_PASSES - 1),
+                )
+            s_sq = work.tile([P, K_PASS], F32, tag="s_sq")
+            nc.scalar.activation(out=s_sq[:], in_=s_ps[:], func=ACT.Square)
+            nc.vector.tensor_tensor(out=a_tiles[j][:, chunk], in0=s_sq[:], in1=s_ps[:], op=ALU.mult)
+            magnitudes = work.tile([P, K_PASS], BF16, tag="magnitudes")
+            nc.scalar.activation(
+                out=magnitudes[:], in_=a_tiles[j][:, chunk], func=ACT.Abs, accum_out=abs_sums[j][:, c : c + 1]
+            )
+
+        def normaliser(j):
+            total = small.tile([P, 1], F32, tag="total")
+            nc.vector.tensor_reduce(out=total[:], in_=abs_sums[j][:], axis=AXIS.X, op=ALU.add)
+            nc.vector.tensor_scalar(out=total[:], in0=total[:], scalar1=EPS, scalar2=None, op0=ALU.max)
+            inv = small.tile([P, 1], F32, tag="inv")
+            nc.vector.reciprocal(out=inv[:], in_=total[:])
+            inv_cols = small.tile([P, P], F32, tag="inv_cols")
+            nc.vector.tensor_scalar(out=inv_cols[:], in0=ones[:], scalar1=inv[:, 0:1], scalar2=None, op0=ALU.mult)
+            inv_ps = psum_m.tile([P, P], F32, tag="m")
+            nc.tensor.transpose(inv_ps[:], inv_cols[:], ident_f32[:])
+            inv_rows[j] = small.tile([P, P], F32, name="inv_rows", tag="inv_rows")
+            nc.vector.tensor_copy(out=inv_rows[j][:], in_=inv_ps[:])
+
+        def transpose_group(j, g):
+            if g == 0:
+                a_grouped[j] = stage.tile([P, N_CHUNKS, P, PACK], BF16, name="a_grouped", tag="a_grouped", align_bytes=64)
+            a_t = psum_t.tile([P, PACK, P], F32, tag="t")
+            for t in range(PACK):
+                first = g * K_PASS + t * P
+                nc.tensor.transpose(a_t[:, t, :], a_tiles[j][:, first : first + P], ident_f32[:])
+            nc.vector.tensor_tensor(
+                out=a_grouped[j][:, g, :, :],
+                in0=a_t[:].rearrange("p t b -> p b t"),
+                in1=inv_rows[j][:].unsqueeze(2).to_broadcast([P, P, PACK]),
+                op=ALU.mult,
+            )
+
+        def echo_and_distances(j):
+            a_codes = stage.tile([P, N_CHUNKS * P], U32, tag="a_codes", align_bytes=64)
+            a_scales = stage.tile([P, N_CHUNKS * P], U8, tag="a_scales", align_bytes=64)
+            nc.vector.quantize_mx(
+                out=a_codes[:].bitcast(FP8X4),
+                scales=a_scales[:],
+                in_=a_grouped[j][:].rearrange("p g b t -> p (g b t)"),
+            )
+            echo_ps = psum_e.tile([P, P], F32, tag="e")
+            for g in range(N_CHUNKS):
+                cols = slice(g * P, (g + 1) * P)
+                nc.tensor.matmul_mx(
+                    out=echo_ps[:],
+                    lhsT=e_codes[:, cols].bitcast(FP8X4),
+                    lhsT_scale=e_scales[:, cols],
+                    rhs=a_codes[:, cols].bitcast(FP8X4),
+                    rhs_scale=a_scales[:, cols],
+                    start=(g == 0),
+                    stop=(g == N_CHUNKS - 1),
+                )
+            echo = small.tile([P, P], F32, tag="echo")
+            nc.scalar.copy(out=echo[:], in_=echo_ps[:])
+            echo_sq = small.tile([P, P], F32, tag="echo_sq")
+            nc.scalar.activation(out=echo_sq[:], in_=echo_ps[:], func=ACT.Square)
+            d_ps = psum_m.tile([P, L_PAD], F32, tag="m")
+            nc.tensor.matmul(out=d_ps[:], lhsT=echo_sq[:], rhs=ones[:, 0:L_PAD], start=True, stop=False)
+            nc.tensor.matmul(out=d_ps[:], lhsT=echo[:], rhs=cls_m2[:], start=False, stop=False)
+            nc.tensor.matmul(out=d_ps[:], lhsT=ones[:], rhs=cls_sq[:], start=False, stop=True)
+            nc.vector.tensor_scalar(out=dist_sq[:, j, :], in0=d_ps[:, 0:L], scalar1=0.0, scalar2=None, op0=ALU.max)
+
+        for first in range(0, UNITS + LAG, RUN):
+            for unit in range(first, min(first + RUN, UNITS)):
+                j, c = divmod(unit, N_CHUNKS)
+                if j == 0:
+                    rows_to_mx(take_block(1 + c), x_codes, x_scales, slice(c * K_PASS, (c + 1) * K_PASS))
+                if unit == N_CHUNKS:
+                    rows_to_mx(take_block(F_BLOCKS[1]), f_codes, f_scales, slice(K_PASS, 2 * K_PASS))
+                    e_raw = take_block(E_BLOCK)[:].rearrange("p (g t c) -> p g c t", g=N_CHUNKS, t=PACK)
+                    e_grouped = stage.tile([P, N_CHUNKS, C, PACK], BF16, tag="grouped", align_bytes=64)
+                    nc.vector.tensor_copy(out=e_grouped[:], in_=e_raw)
+                    nc.vector.quantize_mx(
+                        out=e_codes[:].bitcast(FP8X4),
+                        scales=e_scales[:],
+                        in_=e_grouped[:].rearrange("p g c t -> p (g c t)"),
+                    )
+                similarities(j, c)
+                if c == N_CHUNKS - 1:
+                    normaliser(j)
+            for group in range(max(first - LAG, 0), first - LAG + RUN):
+                j, g = divmod(group, N_CHUNKS)
+                transpose_group(j, g)
+                if g == N_CHUNKS - 1:
+                    echo_and_distances(j)
+
+        dist = keep.tile([P, B_TILES, L], F32)
+        nc.scalar.activation(out=dist[:], in_=dist_sq[:], func=ACT.Sqrt)
+        result = keep.tile([P, B_TILES, L], F32)
+        nc.scalar.mul(out=result[:], in_=dist[:], mul=-1.0)
+        nc.sync.dma_start(out=out.rearrange("(p j) l -> p j l", j=B_TILES), in_=result[:])

@@ -25,12 +25,30 @@ F_PASSES = F // K_PASS
 ROW_TILES = K_PASS // P
 L_PAD = 32
 
-UNITS = B_TILES * N_CHUNKS
 RUN = 2
-LAG = N_CHUNKS + RUN
+STEPS_PER_TILE = N_CHUNKS // RUN
+STEPS = B_TILES * STEPS_PER_TILE
+SUM_LAG = 1
+SPREAD_LAG = 2
+GROUP_LAG = STEPS_PER_TILE + SPREAD_LAG
+ECHO_LAG = GROUP_LAG + 2
+DIST_LAG = GROUP_LAG + 3
 AHEAD = 3
+SCALAR_ROW_TILES = 3
 
 FLOPS = 2 * B * N * F + 2 * B * N * C
+
+
+def units_of(step):
+    if step < 0 or step >= STEPS:
+        return []
+    return [divmod(unit, N_CHUNKS) for unit in range(step * RUN, (step + 1) * RUN)]
+
+
+def tile_ending_at(step):
+    if 0 <= step < STEPS and (step + 1) % STEPS_PER_TILE == 0:
+        return step // STEPS_PER_TILE
+    return None
 
 
 def tile_minerva_old_pb_kernel(tc, f_unit, exf_unit, ex_class_reps, class_reps, out):
@@ -40,13 +58,38 @@ def tile_minerva_old_pb_kernel(tc, f_unit, exf_unit, ex_class_reps, class_reps, 
         keep = stack.enter_context(tc.tile_pool(name="keep", bufs=1))
         raw_pool = stack.enter_context(tc.tile_pool(name="raw", bufs=AHEAD + 1))
         stage = stack.enter_context(tc.tile_pool(name="stage", bufs=2))
+        grouped_pool = stack.enter_context(tc.tile_pool(name="grouped", bufs=4))
         a_pool = stack.enter_context(tc.tile_pool(name="a", bufs=3))
-        work = stack.enter_context(tc.tile_pool(name="work", bufs=3))
+        work = stack.enter_context(tc.tile_pool(name="work", bufs=4))
         small = stack.enter_context(tc.tile_pool(name="small", bufs=2))
         psum_s = stack.enter_context(tc.psum_pool(name="psum_s", bufs=3))
         psum_t = stack.enter_context(tc.psum_pool(name="psum_t", bufs=3))
         psum_e = stack.enter_context(tc.psum_pool(name="psum_e", bufs=1))
         psum_m = stack.enter_context(tc.psum_pool(name="psum_m", bufs=1))
+        stack.enter_context(tc.manual_schedule())
+
+        f_rows = f_unit.rearrange("(p j) k -> p j k", j=B_TILES)
+        blocks = [f_rows[:, 0:ROW_TILES, :]]
+        for c in range(N_CHUNKS):
+            blocks.append(exf_unit[c * K_PASS : (c + 1) * K_PASS, :].rearrange("(p t) k -> p t k", t=PACK))
+        blocks.append(ex_class_reps.rearrange("(g p t) c -> p g (t c)", p=P, t=PACK))
+        blocks.append(f_rows[:, ROW_TILES : 2 * ROW_TILES, :])
+        raw_tiles = {}
+
+        def load_block(i):
+            raw_tiles[i] = raw_pool.tile([P, ROW_TILES * F], BF16, name="raw", tag="raw")
+            nc.sync.dma_start(out=raw_tiles[i][:].rearrange("p (r x) -> p r x", r=blocks[i].shape[1]), in_=blocks[i])
+
+        def take_block(i):
+            if i + AHEAD < len(blocks):
+                load_block(i + AHEAD)
+            return raw_tiles[i]
+
+        for i in range(AHEAD):
+            load_block(i)
+        cls_pad = consts.tile([P, C], BF16)
+        nc.vector.memset(cls_pad[:], 0.0)
+        nc.sync.dma_start(out=cls_pad[0:L, :], in_=class_reps)
 
         ident_f32 = consts.tile([P, P], F32)
         make_identity(nc, ident_f32[:])
@@ -65,28 +108,9 @@ def tile_minerva_old_pb_kernel(tc, f_unit, exf_unit, ex_class_reps, class_reps, 
         e_scales = keep.tile([P, N_CHUNKS * C], U8, align_bytes=64)
         dist_sq = keep.tile([P, B_TILES, L], F32)
 
-        f_rows = f_unit.rearrange("(p j) k -> p j k", j=B_TILES)
-        blocks = [f_rows[:, 0:ROW_TILES, :]]
-        for c in range(N_CHUNKS):
-            blocks.append(exf_unit[c * K_PASS : (c + 1) * K_PASS, :].rearrange("(p t) k -> p t k", t=PACK))
-        blocks.append(f_rows[:, ROW_TILES : 2 * ROW_TILES, :])
-        blocks.append(ex_class_reps.rearrange("(g p t) c -> p g (t c)", p=P, t=PACK))
-        F_BLOCKS = (0, N_CHUNKS + 1)
-        E_BLOCK = N_CHUNKS + 2
-        raw_tiles = {}
-
-        def load_block(i):
-            raw_tiles[i] = raw_pool.tile([P, ROW_TILES * F], BF16, name="raw", tag="raw")
-            nc.sync.dma_start(out=raw_tiles[i][:].rearrange("p (r x) -> p r x", r=blocks[i].shape[1]), in_=blocks[i])
-
-        def take_block(i):
-            if i + AHEAD < len(blocks):
-                load_block(i + AHEAD)
-            return raw_tiles[i]
-
-        def rows_to_mx(raw, codes, scales, cols):
+        def transpose_rows(raw, scalar_row_tiles):
             words = raw[:].bitcast(F32).rearrange("p (r w) -> p r w", r=ROW_TILES)
-            grouped = stage.tile([P, F_PASSES, K_PASS * PACK], BF16, tag="grouped", align_bytes=64)
+            grouped = grouped_pool.tile([P, F_PASSES, K_PASS * PACK], BF16, tag="grouped", align_bytes=64)
             grouped_words = grouped[:].bitcast(F32).rearrange("p g (r m u) -> p g r m u", r=ROW_TILES, u=2)
             for r in range(ROW_TILES):
                 planes = psum_t.tile([P, F_PASSES, 2, P], F32, tag="t")
@@ -94,38 +118,35 @@ def tile_minerva_old_pb_kernel(tc, f_unit, exf_unit, ex_class_reps, class_reps, 
                     for u in range(2):
                         first = (2 * g + u) * P
                         nc.tensor.transpose(planes[:, g, u, :], words[:, r, first : first + P], ident_f32[:])
-                nc.scalar.copy(out=grouped_words[:, :, r, :, :], in_=planes[:].rearrange("p g u m -> p g m u"))
+                if r < scalar_row_tiles:
+                    nc.scalar.copy(out=grouped_words[:, :, r, :, :], in_=planes[:].rearrange("p g u m -> p g m u"))
+                else:
+                    nc.vector.tensor_copy(out=grouped_words[:, :, r, :, :], in_=planes[:].rearrange("p g u m -> p g m u"))
+            return grouped
+
+        def quantise_rows(grouped, codes, scales, cols):
             for g in range(F_PASSES):
                 nc.vector.quantize_mx(
                     out=codes[:, g, cols].bitcast(FP8X4), scales=scales[:, g, cols], in_=grouped[:, g, :]
                 )
 
-        for i in range(AHEAD):
-            load_block(i)
+        def group_class_vectors(raw, e_grouped, half):
+            chunks = slice(half * N_CHUNKS // 2, (half + 1) * N_CHUNKS // 2)
+            e_raw = raw[:].rearrange("p (g t c) -> p g c t", g=N_CHUNKS, t=PACK)
+            nc.vector.tensor_copy(out=e_grouped[:, chunks, :, :], in_=e_raw[:, chunks, :, :])
 
-        cls_pad = consts.tile([P, C], BF16)
-        nc.vector.memset(cls_pad[:], 0.0)
-        nc.sync.dma_start(out=cls_pad[0:L, :], in_=class_reps)
-        cls_ps = psum_m.tile([P, P], BF16, tag="m")
-        nc.tensor.transpose(cls_ps[:], cls_pad[:], ident_bf16[:])
-        cls_t = consts.tile([P, L_PAD], F32)
-        nc.vector.tensor_copy(out=cls_t[:], in_=cls_ps[:, 0:L_PAD])
-        cls_m2 = consts.tile([P, L_PAD], F32)
-        nc.vector.tensor_scalar(out=cls_m2[:], in0=cls_t[:], scalar1=-2.0, scalar2=None, op0=ALU.mult)
-        cls_sq = consts.tile([P, L_PAD], F32)
-        nc.vector.tensor_tensor(out=cls_sq[:], in0=cls_t[:], in1=cls_t[:], op=ALU.mult)
-
-        rows_to_mx(take_block(F_BLOCKS[0]), f_codes, f_scales, slice(0, K_PASS))
-
+        s_banks = {}
+        s_squares = {}
         a_tiles = {}
         abs_sums = {}
+        inv_sums = {}
         inv_rows = {}
+        a_banks = {}
         a_grouped = {}
+        a_mx = {}
+        echoes = {}
 
         def similarities(j, c):
-            if c == 0:
-                a_tiles[j] = a_pool.tile([P, N], F32, name="a_rows", tag="a")
-                abs_sums[j] = small.tile([P, N_CHUNKS], F32, name="abs_sums", tag="abs_sums", bufs=3)
             probes = slice(j * P, (j + 1) * P)
             chunk = slice(c * K_PASS, (c + 1) * K_PASS)
             s_ps = psum_s.tile([P, K_PASS], F32, tag="s")
@@ -141,92 +162,157 @@ def tile_minerva_old_pb_kernel(tc, f_unit, exf_unit, ex_class_reps, class_reps, 
                 )
             s_sq = work.tile([P, K_PASS], F32, tag="s_sq")
             nc.scalar.activation(out=s_sq[:], in_=s_ps[:], func=ACT.Square)
-            nc.vector.tensor_tensor(out=a_tiles[j][:, chunk], in0=s_sq[:], in1=s_ps[:], op=ALU.mult)
-            magnitudes = work.tile([P, K_PASS], BF16, tag="magnitudes")
+            s_banks[j, c] = s_ps
+            s_squares[j, c] = s_sq
+
+        def cube(j, c):
+            if c == 0:
+                a_tiles[j] = a_pool.tile([P, N], F32, name="a_rows", tag="a")
+            chunk = slice(c * K_PASS, (c + 1) * K_PASS)
+            nc.vector.tensor_tensor(out=a_tiles[j][:, chunk], in0=s_squares[j, c][:], in1=s_banks[j, c][:], op=ALU.mult)
+
+        def sum_magnitudes(step):
+            j, i = divmod(step, STEPS_PER_TILE)
+            if i == 0:
+                abs_sums[j] = small.tile([P, STEPS_PER_TILE + 1], F32, name="abs_sums", tag="abs_sums")
+            chunks = slice(i * RUN * K_PASS, (i + 1) * RUN * K_PASS)
+            magnitudes = work.tile([P, RUN * K_PASS], BF16, tag="magnitudes")
             nc.scalar.activation(
-                out=magnitudes[:], in_=a_tiles[j][:, chunk], func=ACT.Abs, accum_out=abs_sums[j][:, c : c + 1]
+                out=magnitudes[:], in_=a_tiles[j][:, chunks], func=ACT.Abs, accum_out=abs_sums[j][:, i : i + 1]
             )
 
-        def normaliser(j):
-            total = small.tile([P, 1], F32, tag="total")
-            nc.vector.tensor_reduce(out=total[:], in_=abs_sums[j][:], axis=AXIS.X, op=ALU.add)
-            nc.vector.tensor_scalar(out=total[:], in0=total[:], scalar1=EPS, scalar2=None, op0=ALU.max)
-            inv = small.tile([P, 1], F32, tag="inv")
-            nc.vector.reciprocal(out=inv[:], in_=total[:])
-            inv_cols = small.tile([P, P], F32, tag="inv_cols")
-            nc.vector.tensor_scalar(out=inv_cols[:], in0=ones[:], scalar1=inv[:, 0:1], scalar2=None, op0=ALU.mult)
-            inv_ps = psum_m.tile([P, P], F32, tag="m")
-            nc.tensor.transpose(inv_ps[:], inv_cols[:], ident_f32[:])
-            inv_rows[j] = small.tile([P, P], F32, name="inv_rows", tag="inv_rows")
-            nc.vector.tensor_copy(out=inv_rows[j][:], in_=inv_ps[:])
-
         def transpose_group(j, g):
-            if g == 0:
-                a_grouped[j] = stage.tile([P, N_CHUNKS, P, PACK], BF16, name="a_grouped", tag="a_grouped", align_bytes=64)
             a_t = psum_t.tile([P, PACK, P], F32, tag="t")
             for t in range(PACK):
                 first = g * K_PASS + t * P
                 nc.tensor.transpose(a_t[:, t, :], a_tiles[j][:, first : first + P], ident_f32[:])
+            a_banks[j, g] = a_t
+
+        def normalise_group(j, g):
+            if g == 0:
+                a_grouped[j] = stage.tile([P, N_CHUNKS, P, PACK], BF16, name="a_grouped", tag="a_grouped", align_bytes=64)
             nc.vector.tensor_tensor(
                 out=a_grouped[j][:, g, :, :],
-                in0=a_t[:].rearrange("p t b -> p b t"),
+                in0=a_banks[j, g][:].rearrange("p t b -> p b t"),
                 in1=inv_rows[j][:].unsqueeze(2).to_broadcast([P, P, PACK]),
                 op=ALU.mult,
             )
 
-        def echo_and_distances(j):
-            a_codes = stage.tile([P, N_CHUNKS * P], U32, tag="a_codes", align_bytes=64)
-            a_scales = stage.tile([P, N_CHUNKS * P], U8, tag="a_scales", align_bytes=64)
-            nc.vector.quantize_mx(
-                out=a_codes[:].bitcast(FP8X4),
-                scales=a_scales[:],
-                in_=a_grouped[j][:].rearrange("p g b t -> p (g b t)"),
-            )
-            echo_ps = psum_e.tile([P, P], F32, tag="e")
-            for g in range(N_CHUNKS):
-                cols = slice(g * P, (g + 1) * P)
-                nc.tensor.matmul_mx(
-                    out=echo_ps[:],
-                    lhsT=e_codes[:, cols].bitcast(FP8X4),
-                    lhsT_scale=e_scales[:, cols],
-                    rhs=a_codes[:, cols].bitcast(FP8X4),
-                    rhs_scale=a_scales[:, cols],
-                    start=(g == 0),
-                    stop=(g == N_CHUNKS - 1),
-                )
-            echo = small.tile([P, P], F32, tag="echo")
-            nc.scalar.copy(out=echo[:], in_=echo_ps[:])
-            echo_sq = small.tile([P, P], F32, tag="echo_sq")
-            nc.scalar.activation(out=echo_sq[:], in_=echo_ps[:], func=ACT.Square)
-            d_ps = psum_m.tile([P, L_PAD], F32, tag="m")
-            nc.tensor.matmul(out=d_ps[:], lhsT=echo_sq[:], rhs=ones[:, 0:L_PAD], start=True, stop=False)
-            nc.tensor.matmul(out=d_ps[:], lhsT=echo[:], rhs=cls_m2[:], start=False, stop=False)
-            nc.tensor.matmul(out=d_ps[:], lhsT=ones[:], rhs=cls_sq[:], start=False, stop=True)
-            nc.vector.tensor_scalar(out=dist_sq[:, j, :], in0=d_ps[:, 0:L], scalar1=0.0, scalar2=None, op0=ALU.max)
+        x_grouped = {}
+        f_grouped = transpose_rows(take_block(0), SCALAR_ROW_TILES)
+        for j, c in units_of(0):
+            x_grouped[c] = transpose_rows(take_block(1 + c), SCALAR_ROW_TILES)
+        quantise_rows(f_grouped, f_codes, f_scales, slice(0, K_PASS))
+        for j, c in units_of(0):
+            quantise_rows(x_grouped[c], x_codes, x_scales, slice(c * K_PASS, (c + 1) * K_PASS))
+        for j, c in units_of(1):
+            x_grouped[c] = transpose_rows(take_block(1 + c), SCALAR_ROW_TILES)
 
-        for first in range(0, UNITS + LAG, RUN):
-            for unit in range(first, min(first + RUN, UNITS)):
-                j, c = divmod(unit, N_CHUNKS)
-                if j == 0:
-                    rows_to_mx(take_block(1 + c), x_codes, x_scales, slice(c * K_PASS, (c + 1) * K_PASS))
-                if unit == N_CHUNKS:
-                    rows_to_mx(take_block(F_BLOCKS[1]), f_codes, f_scales, slice(K_PASS, 2 * K_PASS))
-                    e_raw = take_block(E_BLOCK)[:].rearrange("p (g t c) -> p g c t", g=N_CHUNKS, t=PACK)
-                    e_grouped = stage.tile([P, N_CHUNKS, C, PACK], BF16, tag="grouped", align_bytes=64)
-                    nc.vector.tensor_copy(out=e_grouped[:], in_=e_raw)
-                    nc.vector.quantize_mx(
-                        out=e_codes[:].bitcast(FP8X4),
-                        scales=e_scales[:],
-                        in_=e_grouped[:].rearrange("p g c t -> p (g c t)"),
-                    )
+        cls_ps = psum_m.tile([P, P], BF16, tag="m")
+        nc.tensor.transpose(cls_ps[:], cls_pad[:], ident_bf16[:])
+        cls_t = consts.tile([P, L_PAD], F32)
+        nc.vector.tensor_copy(out=cls_t[:], in_=cls_ps[:, 0:L_PAD])
+        cls_m2 = consts.tile([P, L_PAD], F32)
+        nc.vector.tensor_scalar(out=cls_m2[:], in0=cls_t[:], scalar1=-2.0, scalar2=None, op0=ALU.mult)
+        cls_sq = consts.tile([P, L_PAD], F32)
+        nc.vector.tensor_tensor(out=cls_sq[:], in0=cls_t[:], in1=cls_t[:], op=ALU.mult)
+
+        for step in range(STEPS + DIST_LAG + 1):
+            j = tile_ending_at(step - SPREAD_LAG)
+            if j is not None:
+                inv_cols = small.tile([P, P], F32, tag="inv_cols")
+                nc.vector.tensor_scalar(
+                    out=inv_cols[:], in0=ones[:], scalar1=inv_sums[j][:, 0:1], scalar2=1.0 / EPS, op0=ALU.mult, op1=ALU.min
+                )
+
+            for j, c in units_of(step):
                 similarities(j, c)
-                if c == N_CHUNKS - 1:
-                    normaliser(j)
-            for group in range(max(first - LAG, 0), first - LAG + RUN):
-                j, g = divmod(group, N_CHUNKS)
+            if step + 1 < STEPS_PER_TILE:
+                for j, c in units_of(step + 1):
+                    quantise_rows(x_grouped[c], x_codes, x_scales, slice(c * K_PASS, (c + 1) * K_PASS))
+            for j, c in units_of(step):
+                cube(j, c)
+
+            if step + 2 < STEPS_PER_TILE:
+                for j, c in units_of(step + 2):
+                    x_grouped[c] = transpose_rows(take_block(1 + c), SCALAR_ROW_TILES)
+
+            for j, g in units_of(step - GROUP_LAG):
                 transpose_group(j, g)
-                if g == N_CHUNKS - 1:
-                    echo_and_distances(j)
+            j = tile_ending_at(step - SPREAD_LAG)
+            if j is not None:
+                inv_ps = psum_m.tile([P, P], F32, tag="m")
+                nc.tensor.transpose(inv_ps[:], inv_cols[:], ident_f32[:])
+            for j, g in units_of(step - GROUP_LAG):
+                normalise_group(j, g)
+
+            if step == STEPS_PER_TILE - 1:
+                e_raw = take_block(1 + N_CHUNKS)
+                e_grouped = grouped_pool.tile([P, N_CHUNKS, C, PACK], BF16, tag="grouped", align_bytes=64)
+                group_class_vectors(e_raw, e_grouped, 0)
+            if step == STEPS_PER_TILE:
+                group_class_vectors(e_raw, e_grouped, 1)
+                f_grouped = transpose_rows(take_block(2 + N_CHUNKS), 0)
+            if step == STEPS_PER_TILE + 1:
+                nc.vector.quantize_mx(
+                    out=e_codes[:].bitcast(FP8X4), scales=e_scales[:], in_=e_grouped[:].rearrange("p g c t -> p (g c t)")
+                )
+                quantise_rows(f_grouped, f_codes, f_scales, slice(K_PASS, 2 * K_PASS))
+
+            if 0 <= step - SUM_LAG < STEPS:
+                sum_magnitudes(step - SUM_LAG)
+            j = tile_ending_at(step - SUM_LAG)
+            if j is not None:
+                sums_copy = small.tile([P, STEPS_PER_TILE], F32, tag="sums_copy")
+                nc.scalar.activation(
+                    out=sums_copy[:], in_=abs_sums[j][:, 0:STEPS_PER_TILE], func=ACT.Copy,
+                    accum_out=abs_sums[j][:, STEPS_PER_TILE : STEPS_PER_TILE + 1],
+                )
+                inv_sums[j] = small.tile([P, 1], F32, name="inv_sum", tag="inv_sum")
+                nc.vector.reciprocal(out=inv_sums[j][:], in_=abs_sums[j][:, STEPS_PER_TILE : STEPS_PER_TILE + 1])
+            j = tile_ending_at(step - SPREAD_LAG)
+            if j is not None:
+                inv_rows[j] = small.tile([P, P], F32, name="inv_rows", tag="inv_rows")
+                nc.scalar.copy(out=inv_rows[j][:], in_=inv_ps[:])
+
+            j = tile_ending_at(step - GROUP_LAG)
+            if j is not None:
+                a_codes = stage.tile([P, N_CHUNKS * P], U32, tag="a_codes", align_bytes=64)
+                a_scales = stage.tile([P, N_CHUNKS * P], U8, tag="a_scales", align_bytes=64)
+                nc.vector.quantize_mx(
+                    out=a_codes[:].bitcast(FP8X4), scales=a_scales[:], in_=a_grouped[j][:].rearrange("p g b t -> p (g b t)")
+                )
+                a_mx[j] = (a_codes, a_scales)
+
+            j = tile_ending_at(step - ECHO_LAG)
+            if j is not None:
+                a_codes, a_scales = a_mx[j]
+                echo_ps = psum_e.tile([P, P], F32, tag="e")
+                for g in range(N_CHUNKS):
+                    cols = slice(g * P, (g + 1) * P)
+                    nc.tensor.matmul_mx(
+                        out=echo_ps[:],
+                        lhsT=e_codes[:, cols].bitcast(FP8X4),
+                        lhsT_scale=e_scales[:, cols],
+                        rhs=a_codes[:, cols].bitcast(FP8X4),
+                        rhs_scale=a_scales[:, cols],
+                        start=(g == 0),
+                        stop=(g == N_CHUNKS - 1),
+                    )
+                echo = small.tile([P, P], F32, tag="echo")
+                nc.scalar.copy(out=echo[:], in_=echo_ps[:])
+                echo_sq = small.tile([P, P], F32, tag="echo_sq")
+                nc.scalar.activation(out=echo_sq[:], in_=echo_ps[:], func=ACT.Square)
+                echoes[j] = (echo, echo_sq)
+
+            j = tile_ending_at(step - DIST_LAG)
+            if j is not None:
+                echo, echo_sq = echoes[j]
+                d_ps = psum_m.tile([P, L_PAD], F32, tag="m")
+                nc.tensor.matmul(out=d_ps[:], lhsT=echo_sq[:], rhs=ones[:, 0:L_PAD], start=True, stop=False)
+                nc.tensor.matmul(out=d_ps[:], lhsT=echo[:], rhs=cls_m2[:], start=False, stop=False)
+                nc.tensor.matmul(out=d_ps[:], lhsT=ones[:], rhs=cls_sq[:], start=False, stop=True)
+                nc.vector.tensor_scalar(out=dist_sq[:, j, :], in0=d_ps[:, 0:L], scalar1=0.0, scalar2=None, op0=ALU.max)
 
         dist = keep.tile([P, B_TILES, L], F32)
         nc.scalar.activation(out=dist[:], in_=dist_sq[:], func=ACT.Sqrt)

@@ -33,6 +33,10 @@ SPREAD_LAG = 2
 GROUP_LAG = STEPS_PER_TILE + SPREAD_LAG
 ECHO_LAG = GROUP_LAG + 2
 DIST_LAG = GROUP_LAG + 3
+E_STEP = STEPS_PER_TILE
+E_PIECES = 4
+F_STEP = 2 * STEPS_PER_TILE
+PREPARE_AHEAD = 3
 AHEAD = 3
 SCALAR_ROW_TILES = 3
 
@@ -63,8 +67,7 @@ def tile_minerva_old_pb_kernel(tc, f_unit, exf_unit, ex_class_reps, class_reps, 
         work = stack.enter_context(tc.tile_pool(name="work", bufs=4))
         small = stack.enter_context(tc.tile_pool(name="small", bufs=2))
         psum_s = stack.enter_context(tc.psum_pool(name="psum_s", bufs=3))
-        psum_t = stack.enter_context(tc.psum_pool(name="psum_t", bufs=3))
-        psum_e = stack.enter_context(tc.psum_pool(name="psum_e", bufs=1))
+        psum_t = stack.enter_context(tc.psum_pool(name="psum_t", bufs=4))
         psum_m = stack.enter_context(tc.psum_pool(name="psum_m", bufs=1))
         stack.enter_context(tc.manual_schedule())
 
@@ -109,20 +112,23 @@ def tile_minerva_old_pb_kernel(tc, f_unit, exf_unit, ex_class_reps, class_reps, 
         dist_sq = keep.tile([P, B_TILES, L], F32)
 
         def transpose_rows(raw, scalar_row_tiles):
-            words = raw[:].bitcast(F32).rearrange("p (r w) -> p r w", r=ROW_TILES)
             grouped = grouped_pool.tile([P, F_PASSES, K_PASS * PACK], BF16, tag="grouped", align_bytes=64)
-            grouped_words = grouped[:].bitcast(F32).rearrange("p g (r m u) -> p g r m u", r=ROW_TILES, u=2)
             for r in range(ROW_TILES):
-                planes = psum_t.tile([P, F_PASSES, 2, P], F32, tag="t")
-                for g in range(F_PASSES):
-                    for u in range(2):
-                        first = (2 * g + u) * P
-                        nc.tensor.transpose(planes[:, g, u, :], words[:, r, first : first + P], ident_f32[:])
-                if r < scalar_row_tiles:
-                    nc.scalar.copy(out=grouped_words[:, :, r, :, :], in_=planes[:].rearrange("p g u m -> p g m u"))
-                else:
-                    nc.vector.tensor_copy(out=grouped_words[:, :, r, :, :], in_=planes[:].rearrange("p g u m -> p g m u"))
+                transpose_row_tile(raw, grouped, r, r < scalar_row_tiles)
             return grouped
+
+        def transpose_row_tile(raw, grouped, r, on_scalar):
+            words = raw[:].bitcast(F32).rearrange("p (r w) -> p r w", r=ROW_TILES)
+            grouped_words = grouped[:].bitcast(F32).rearrange("p g (r m u) -> p g r m u", r=ROW_TILES, u=2)
+            planes = psum_t.tile([P, F_PASSES, 2, P], F32, tag="t")
+            for g in range(F_PASSES):
+                for u in range(2):
+                    first = (2 * g + u) * P
+                    nc.tensor.transpose(planes[:, g, u, :], words[:, r, first : first + P], ident_f32[:])
+            if on_scalar:
+                nc.scalar.copy(out=grouped_words[:, :, r, :, :], in_=planes[:].rearrange("p g u m -> p g m u"))
+            else:
+                nc.vector.tensor_copy(out=grouped_words[:, :, r, :, :], in_=planes[:].rearrange("p g u m -> p g m u"))
 
         def quantise_rows(grouped, codes, scales, cols):
             for g in range(F_PASSES):
@@ -130,8 +136,8 @@ def tile_minerva_old_pb_kernel(tc, f_unit, exf_unit, ex_class_reps, class_reps, 
                     out=codes[:, g, cols].bitcast(FP8X4), scales=scales[:, g, cols], in_=grouped[:, g, :]
                 )
 
-        def group_class_vectors(raw, e_grouped, half):
-            chunks = slice(half * N_CHUNKS // 2, (half + 1) * N_CHUNKS // 2)
+        def group_class_vectors(raw, e_grouped, i):
+            chunks = slice(i * N_CHUNKS // E_PIECES, (i + 1) * N_CHUNKS // E_PIECES)
             e_raw = raw[:].rearrange("p (g t c) -> p g c t", g=N_CHUNKS, t=PACK)
             nc.vector.tensor_copy(out=e_grouped[:, chunks, :, :], in_=e_raw[:, chunks, :, :])
 
@@ -199,14 +205,18 @@ def tile_minerva_old_pb_kernel(tc, f_unit, exf_unit, ex_class_reps, class_reps, 
             )
 
         x_grouped = {}
+
+        def prepare_exemplars(c):
+            if 0 < c <= N_CHUNKS:
+                quantise_rows(x_grouped[c - 1], x_codes, x_scales, slice((c - 1) * K_PASS, c * K_PASS))
+            if c < N_CHUNKS:
+                x_grouped[c] = transpose_rows(take_block(1 + c), SCALAR_ROW_TILES)
+
         f_grouped = transpose_rows(take_block(0), SCALAR_ROW_TILES)
-        for j, c in units_of(0):
-            x_grouped[c] = transpose_rows(take_block(1 + c), SCALAR_ROW_TILES)
+        prepare_exemplars(0)
         quantise_rows(f_grouped, f_codes, f_scales, slice(0, K_PASS))
-        for j, c in units_of(0):
-            quantise_rows(x_grouped[c], x_codes, x_scales, slice(c * K_PASS, (c + 1) * K_PASS))
-        for j, c in units_of(1):
-            x_grouped[c] = transpose_rows(take_block(1 + c), SCALAR_ROW_TILES)
+        for c in range(1, PREPARE_AHEAD):
+            prepare_exemplars(c)
 
         cls_ps = psum_m.tile([P, P], BF16, tag="m")
         nc.tensor.transpose(cls_ps[:], cls_pad[:], ident_bf16[:])
@@ -227,37 +237,25 @@ def tile_minerva_old_pb_kernel(tc, f_unit, exf_unit, ex_class_reps, class_reps, 
 
             for j, c in units_of(step):
                 similarities(j, c)
-            if step + 1 < STEPS_PER_TILE:
-                for j, c in units_of(step + 1):
-                    quantise_rows(x_grouped[c], x_codes, x_scales, slice(c * K_PASS, (c + 1) * K_PASS))
+                if j == 0:
+                    prepare_exemplars(c + PREPARE_AHEAD)
             for j, c in units_of(step):
                 cube(j, c)
 
-            if step + 2 < STEPS_PER_TILE:
-                for j, c in units_of(step + 2):
-                    x_grouped[c] = transpose_rows(take_block(1 + c), SCALAR_ROW_TILES)
-
             for j, g in units_of(step - GROUP_LAG):
                 transpose_group(j, g)
+            r = step - F_STEP
+            if r == 0:
+                f_raw = take_block(2 + N_CHUNKS)
+                f_grouped = grouped_pool.tile([P, F_PASSES, K_PASS * PACK], BF16, tag="grouped", align_bytes=64)
+            if 0 <= r < ROW_TILES:
+                transpose_row_tile(f_raw, f_grouped, r, True)
             j = tile_ending_at(step - SPREAD_LAG)
             if j is not None:
                 inv_ps = psum_m.tile([P, P], F32, tag="m")
                 nc.tensor.transpose(inv_ps[:], inv_cols[:], ident_f32[:])
             for j, g in units_of(step - GROUP_LAG):
                 normalise_group(j, g)
-
-            if step == STEPS_PER_TILE - 1:
-                e_raw = take_block(1 + N_CHUNKS)
-                e_grouped = grouped_pool.tile([P, N_CHUNKS, C, PACK], BF16, tag="grouped", align_bytes=64)
-                group_class_vectors(e_raw, e_grouped, 0)
-            if step == STEPS_PER_TILE:
-                group_class_vectors(e_raw, e_grouped, 1)
-                f_grouped = transpose_rows(take_block(2 + N_CHUNKS), 0)
-            if step == STEPS_PER_TILE + 1:
-                nc.vector.quantize_mx(
-                    out=e_codes[:].bitcast(FP8X4), scales=e_scales[:], in_=e_grouped[:].rearrange("p g c t -> p (g c t)")
-                )
-                quantise_rows(f_grouped, f_codes, f_scales, slice(K_PASS, 2 * K_PASS))
 
             if 0 <= step - SUM_LAG < STEPS:
                 sum_magnitudes(step - SUM_LAG)
@@ -284,10 +282,23 @@ def tile_minerva_old_pb_kernel(tc, f_unit, exf_unit, ex_class_reps, class_reps, 
                 )
                 a_mx[j] = (a_codes, a_scales)
 
+            i = step - E_STEP
+            if i == 0:
+                e_raw = take_block(1 + N_CHUNKS)
+                e_grouped = grouped_pool.tile([P, N_CHUNKS, C, PACK], BF16, tag="grouped", align_bytes=64)
+            if 0 <= i < E_PIECES:
+                group_class_vectors(e_raw, e_grouped, i)
+            if i == E_PIECES:
+                nc.vector.quantize_mx(
+                    out=e_codes[:].bitcast(FP8X4), scales=e_scales[:], in_=e_grouped[:].rearrange("p g c t -> p (g c t)")
+                )
+            if step == F_STEP + ROW_TILES:
+                quantise_rows(f_grouped, f_codes, f_scales, slice(K_PASS, 2 * K_PASS))
+
             j = tile_ending_at(step - ECHO_LAG)
             if j is not None:
                 a_codes, a_scales = a_mx[j]
-                echo_ps = psum_e.tile([P, P], F32, tag="e")
+                echo_ps = psum_m.tile([P, P], F32, tag="m")
                 for g in range(N_CHUNKS):
                     cols = slice(g * P, (g + 1) * P)
                     nc.tensor.matmul_mx(
@@ -312,7 +323,7 @@ def tile_minerva_old_pb_kernel(tc, f_unit, exf_unit, ex_class_reps, class_reps, 
                 nc.tensor.matmul(out=d_ps[:], lhsT=echo_sq[:], rhs=ones[:, 0:L_PAD], start=True, stop=False)
                 nc.tensor.matmul(out=d_ps[:], lhsT=echo[:], rhs=cls_m2[:], start=False, stop=False)
                 nc.tensor.matmul(out=d_ps[:], lhsT=ones[:], rhs=cls_sq[:], start=False, stop=True)
-                nc.vector.tensor_scalar(out=dist_sq[:, j, :], in0=d_ps[:, 0:L], scalar1=0.0, scalar2=None, op0=ALU.max)
+                nc.scalar.activation(out=dist_sq[:, j, :], in_=d_ps[:, 0:L], func=ACT.Relu)
 
         dist = keep.tile([P, B_TILES, L], F32)
         nc.scalar.activation(out=dist[:], in_=dist_sq[:], func=ACT.Sqrt)

@@ -28,11 +28,13 @@ L_PAD = 32
 RUN = 2
 STEPS_PER_TILE = N_CHUNKS // RUN
 STEPS = B_TILES * STEPS_PER_TILE
+HALF_STEPS = STEPS_PER_TILE // 2
 SUM_LAG = 1
 SPREAD_LAG = 2
 GROUP_LAG = STEPS_PER_TILE + SPREAD_LAG
-ECHO_LAG = GROUP_LAG + 2
-DIST_LAG = GROUP_LAG + 3
+QUANT_LAG = GROUP_LAG + 1
+ECHO_LAG = GROUP_LAG + 3
+DIST_LAG = GROUP_LAG + 5
 E_STEP = STEPS_PER_TILE
 E_PIECES = 4
 F_STEP = 2 * STEPS_PER_TILE
@@ -204,6 +206,21 @@ def tile_minerva_old_pb_kernel(tc, f_unit, exf_unit, ex_class_reps, class_reps, 
                 op=ALU.mult,
             )
 
+        def quantise_half(j, h):
+            if h == 0:
+                a_mx[j] = (
+                    stage.tile([P, N_CHUNKS * P], U32, name="a_codes", tag="a_codes", align_bytes=64),
+                    stage.tile([P, N_CHUNKS * P], U8, name="a_scales", tag="a_scales", align_bytes=64),
+                )
+            a_codes, a_scales = a_mx[j]
+            chunks = slice(h * N_CHUNKS // 2, (h + 1) * N_CHUNKS // 2)
+            words = slice(h * N_CHUNKS // 2 * P, (h + 1) * N_CHUNKS // 2 * P)
+            nc.vector.quantize_mx(
+                out=a_codes[:, words].bitcast(FP8X4),
+                scales=a_scales[:, words],
+                in_=a_grouped[j][:, chunks, :, :].rearrange("p g b t -> p (g b t)"),
+            )
+
         x_grouped = {}
 
         def prepare_exemplars(c):
@@ -228,11 +245,15 @@ def tile_minerva_old_pb_kernel(tc, f_unit, exf_unit, ex_class_reps, class_reps, 
         nc.vector.tensor_tensor(out=cls_sq[:], in0=cls_t[:], in1=cls_t[:], op=ALU.mult)
 
         for step in range(STEPS + DIST_LAG + 1):
-            j = tile_ending_at(step - SPREAD_LAG)
-            if j is not None:
+            summed = tile_ending_at(step - SUM_LAG)
+            spread = tile_ending_at(step - SPREAD_LAG)
+            groups = units_of(step - GROUP_LAG)
+
+            if spread is not None:
                 inv_cols = small.tile([P, P], F32, tag="inv_cols")
                 nc.vector.tensor_scalar(
-                    out=inv_cols[:], in0=ones[:], scalar1=inv_sums[j][:, 0:1], scalar2=1.0 / EPS, op0=ALU.mult, op1=ALU.min
+                    out=inv_cols[:], in0=ones[:], scalar1=inv_sums[spread][:, 0:1], scalar2=1.0 / EPS,
+                    op0=ALU.mult, op1=ALU.min,
                 )
 
             for j, c in units_of(step):
@@ -241,8 +262,19 @@ def tile_minerva_old_pb_kernel(tc, f_unit, exf_unit, ex_class_reps, class_reps, 
                     prepare_exemplars(c + PREPARE_AHEAD)
             for j, c in units_of(step):
                 cube(j, c)
+            if 0 <= step - QUANT_LAG < STEPS and (step - QUANT_LAG + 1) % HALF_STEPS == 0:
+                quantise_half(*divmod((step - QUANT_LAG) // HALF_STEPS, 2))
 
-            for j, g in units_of(step - GROUP_LAG):
+            if 0 <= step - SUM_LAG < STEPS:
+                sum_magnitudes(step - SUM_LAG)
+            if summed is not None:
+                sums_copy = small.tile([P, STEPS_PER_TILE], F32, tag="sums_copy")
+                nc.scalar.activation(
+                    out=sums_copy[:], in_=abs_sums[summed][:, 0:STEPS_PER_TILE], func=ACT.Copy,
+                    accum_out=abs_sums[summed][:, STEPS_PER_TILE : STEPS_PER_TILE + 1],
+                )
+
+            for j, g in groups:
                 transpose_group(j, g)
             r = step - F_STEP
             if r == 0:
@@ -250,37 +282,22 @@ def tile_minerva_old_pb_kernel(tc, f_unit, exf_unit, ex_class_reps, class_reps, 
                 f_grouped = grouped_pool.tile([P, F_PASSES, K_PASS * PACK], BF16, tag="grouped", align_bytes=64)
             if 0 <= r < ROW_TILES:
                 transpose_row_tile(f_raw, f_grouped, r, True)
-            j = tile_ending_at(step - SPREAD_LAG)
-            if j is not None:
+            if spread is not None:
                 inv_ps = psum_m.tile([P, P], F32, tag="m")
                 nc.tensor.transpose(inv_ps[:], inv_cols[:], ident_f32[:])
-            for j, g in units_of(step - GROUP_LAG):
+
+            for j, g in groups[:1]:
                 normalise_group(j, g)
-
-            if 0 <= step - SUM_LAG < STEPS:
-                sum_magnitudes(step - SUM_LAG)
-            j = tile_ending_at(step - SUM_LAG)
-            if j is not None:
-                sums_copy = small.tile([P, STEPS_PER_TILE], F32, tag="sums_copy")
-                nc.scalar.activation(
-                    out=sums_copy[:], in_=abs_sums[j][:, 0:STEPS_PER_TILE], func=ACT.Copy,
-                    accum_out=abs_sums[j][:, STEPS_PER_TILE : STEPS_PER_TILE + 1],
+            if summed is not None:
+                inv_sums[summed] = small.tile([P, 1], F32, name="inv_sum", tag="inv_sum")
+                nc.vector.reciprocal(
+                    out=inv_sums[summed][:], in_=abs_sums[summed][:, STEPS_PER_TILE : STEPS_PER_TILE + 1]
                 )
-                inv_sums[j] = small.tile([P, 1], F32, name="inv_sum", tag="inv_sum")
-                nc.vector.reciprocal(out=inv_sums[j][:], in_=abs_sums[j][:, STEPS_PER_TILE : STEPS_PER_TILE + 1])
-            j = tile_ending_at(step - SPREAD_LAG)
-            if j is not None:
-                inv_rows[j] = small.tile([P, P], F32, name="inv_rows", tag="inv_rows")
-                nc.scalar.copy(out=inv_rows[j][:], in_=inv_ps[:])
-
-            j = tile_ending_at(step - GROUP_LAG)
-            if j is not None:
-                a_codes = stage.tile([P, N_CHUNKS * P], U32, tag="a_codes", align_bytes=64)
-                a_scales = stage.tile([P, N_CHUNKS * P], U8, tag="a_scales", align_bytes=64)
-                nc.vector.quantize_mx(
-                    out=a_codes[:].bitcast(FP8X4), scales=a_scales[:], in_=a_grouped[j][:].rearrange("p g b t -> p (g b t)")
-                )
-                a_mx[j] = (a_codes, a_scales)
+            for j, g in groups[1:]:
+                normalise_group(j, g)
+            if spread is not None:
+                inv_rows[spread] = small.tile([P, P], F32, name="inv_rows", tag="inv_rows")
+                nc.scalar.copy(out=inv_rows[spread][:], in_=inv_ps[:])
 
             i = step - E_STEP
             if i == 0:
@@ -328,5 +345,5 @@ def tile_minerva_old_pb_kernel(tc, f_unit, exf_unit, ex_class_reps, class_reps, 
         dist = keep.tile([P, B_TILES, L], F32)
         nc.scalar.activation(out=dist[:], in_=dist_sq[:], func=ACT.Sqrt)
         result = keep.tile([P, B_TILES, L], F32)
-        nc.scalar.mul(out=result[:], in_=dist[:], mul=-1.0)
+        nc.vector.tensor_scalar(out=result[:], in0=dist[:], scalar1=-1.0, scalar2=None, op0=ALU.mult)
         nc.sync.dma_start(out=out.rearrange("(p j) l -> p j l", j=B_TILES), in_=result[:])

@@ -28,19 +28,22 @@ L_PAD = 32
 RUN = 2
 STEPS_PER_TILE = N_CHUNKS // RUN
 STEPS = B_TILES * STEPS_PER_TILE
+LAST_TILE_STEP = STEPS - STEPS_PER_TILE
 HALF_STEPS = STEPS_PER_TILE // 2
 SUM_LAG = 1
-SPREAD_LAG = 2
-GROUP_LAG = STEPS_PER_TILE + SPREAD_LAG
+NORM_LAG = STEPS_PER_TILE + SUM_LAG
+GROUP_LAG = NORM_LAG + 1
 QUANT_LAG = GROUP_LAG + 1
 ECHO_LAG = GROUP_LAG + 3
-DIST_LAG = GROUP_LAG + 5
-E_STEP = STEPS_PER_TILE
+DIST_LAG = ECHO_LAG + 1
+F_PIECES = ((0, 1), (1, 1), (2, 2), (4, 4))
+E_STEP = STEPS_PER_TILE - 1
 E_PIECES = 4
+E_QUANT_STEP = E_STEP + 3
 F_STEP = 2 * STEPS_PER_TILE
 PREPARE_AHEAD = 3
 AHEAD = 3
-SCALAR_ROW_TILES = 3
+SCALAR_SHARE = (3, 4)
 
 FLOPS = 2 * B * N * F + 2 * B * N * C
 
@@ -64,26 +67,29 @@ def tile_minerva_old_pb_kernel(tc, f_unit, exf_unit, ex_class_reps, class_reps, 
         keep = stack.enter_context(tc.tile_pool(name="keep", bufs=1))
         raw_pool = stack.enter_context(tc.tile_pool(name="raw", bufs=AHEAD + 1))
         stage = stack.enter_context(tc.tile_pool(name="stage", bufs=2))
-        grouped_pool = stack.enter_context(tc.tile_pool(name="grouped", bufs=4))
+        grouped_pool = stack.enter_context(tc.tile_pool(name="grouped", bufs=3))
         a_pool = stack.enter_context(tc.tile_pool(name="a", bufs=3))
         work = stack.enter_context(tc.tile_pool(name="work", bufs=4))
+        junk = stack.enter_context(tc.tile_pool(name="junk", bufs=2))
         small = stack.enter_context(tc.tile_pool(name="small", bufs=2))
-        psum_s = stack.enter_context(tc.psum_pool(name="psum_s", bufs=3))
+        psum_s = stack.enter_context(tc.psum_pool(name="psum_s", bufs=4))
         psum_t = stack.enter_context(tc.psum_pool(name="psum_t", bufs=4))
-        psum_m = stack.enter_context(tc.psum_pool(name="psum_m", bufs=1))
         stack.enter_context(tc.manual_schedule())
 
         f_rows = f_unit.rearrange("(p j) k -> p j k", j=B_TILES)
-        blocks = [f_rows[:, 0:ROW_TILES, :]]
-        for c in range(N_CHUNKS):
-            blocks.append(exf_unit[c * K_PASS : (c + 1) * K_PASS, :].rearrange("(p t) k -> p t k", t=PACK))
-        blocks.append(ex_class_reps.rearrange("(g p t) c -> p g (t c)", p=P, t=PACK))
-        blocks.append(f_rows[:, ROW_TILES : 2 * ROW_TILES, :])
+        f_blocks = [f_rows[:, first : first + tiles, :] for first, tiles in F_PIECES]
+        x_blocks = [
+            exf_unit[c * K_PASS : (c + 1) * K_PASS, :].rearrange("(p t) k -> p t k", t=PACK) for c in range(N_CHUNKS)
+        ]
+        e_block = ex_class_reps.rearrange("(g p t) c -> p g (t c)", p=P, t=PACK)
+        blocks = f_blocks[0:1] + x_blocks + f_blocks[1:3] + [e_block] + f_blocks[3:4]
+        E_BLOCK = len(blocks) - 2
         raw_tiles = {}
 
         def load_block(i):
             raw_tiles[i] = raw_pool.tile([P, ROW_TILES * F], BF16, name="raw", tag="raw")
-            nc.sync.dma_start(out=raw_tiles[i][:].rearrange("p (r x) -> p r x", r=blocks[i].shape[1]), in_=blocks[i])
+            rows, width = blocks[i].shape[1], blocks[i].shape[2]
+            nc.sync.dma_start(out=raw_tiles[i][:, 0 : rows * width].rearrange("p (r x) -> p r x", r=rows), in_=blocks[i])
 
         def take_block(i):
             if i + AHEAD < len(blocks):
@@ -112,47 +118,101 @@ def tile_minerva_old_pb_kernel(tc, f_unit, exf_unit, ex_class_reps, class_reps, 
         e_codes = keep.tile([P, N_CHUNKS * C], U32, align_bytes=64)
         e_scales = keep.tile([P, N_CHUNKS * C], U8, align_bytes=64)
         dist_sq = keep.tile([P, B_TILES, L], F32)
+        dist = keep.tile([P, B_TILES, L], F32)
+        result = keep.tile([P, B_TILES, L], F32)
 
-        def transpose_rows(raw, scalar_row_tiles):
-            grouped = grouped_pool.tile([P, F_PASSES, K_PASS * PACK], BF16, tag="grouped", align_bytes=64)
-            for r in range(ROW_TILES):
-                transpose_row_tile(raw, grouped, r, r < scalar_row_tiles)
-            return grouped
+        banks_copied = [0]
 
-        def transpose_row_tile(raw, grouped, r, on_scalar):
+        def copy_shared(out, in_):
+            on_scalar = banks_copied[0] * SCALAR_SHARE[0] % SCALAR_SHARE[1] < SCALAR_SHARE[0]
+            banks_copied[0] += 1
+            if on_scalar:
+                nc.scalar.copy(out=out, in_=in_)
+            else:
+                nc.vector.tensor_copy(out=out, in_=in_)
+
+        def new_grouped():
+            return grouped_pool.tile([P, F_PASSES, K_PASS * PACK], BF16, name="grouped", tag="grouped", align_bytes=64)
+
+        def transpose_probe_tile(raw, grouped, tiles, r, copy):
             words = raw[:].bitcast(F32).rearrange("p (r w) -> p r w", r=ROW_TILES)
-            grouped_words = grouped[:].bitcast(F32).rearrange("p g (r m u) -> p g r m u", r=ROW_TILES, u=2)
+            grouped_words = grouped[:].bitcast(F32)[:, :, 0 : tiles * P * 2].rearrange("p g (r m u) -> p g r m u", r=tiles, u=2)
             planes = psum_t.tile([P, F_PASSES, 2, P], F32, tag="t")
             for g in range(F_PASSES):
                 for u in range(2):
                     first = (2 * g + u) * P
                     nc.tensor.transpose(planes[:, g, u, :], words[:, r, first : first + P], ident_f32[:])
-            if on_scalar:
-                nc.scalar.copy(out=grouped_words[:, :, r, :, :], in_=planes[:].rearrange("p g u m -> p g m u"))
-            else:
-                nc.vector.tensor_copy(out=grouped_words[:, :, r, :, :], in_=planes[:].rearrange("p g u m -> p g m u"))
+            copy(out=grouped_words[:, :, r, :, :], in_=planes[:].rearrange("p g u m -> p g m u"))
 
-        def quantise_rows(grouped, codes, scales, cols):
+        def quantise_probes(grouped, piece):
+            first, tiles = F_PIECES[piece]
+            for g in range(F_PASSES):
+                cols = slice(first * P, (first + tiles) * P)
+                nc.vector.quantize_mx(
+                    out=f_codes[:, g, cols].bitcast(FP8X4), scales=f_scales[:, g, cols], in_=grouped[:, g, 0 : tiles * K_PASS]
+                )
+
+        def transpose_exemplars(raw, grouped):
+            words = raw[:].bitcast(F32).rearrange("p (r w) -> p r w", r=ROW_TILES)
+            grouped_words = grouped[:].bitcast(F32).rearrange("p g (h m e u) -> p g h m e u", h=2, e=2, u=2)
+            for g in range(F_PASSES):
+                for h in range(2):
+                    planes = psum_t.tile([P, 2, 2, P], F32, tag="t")
+                    for e in range(2):
+                        for u in range(2):
+                            first = (2 * g + u) * P
+                            nc.tensor.transpose(planes[:, e, u, :], words[:, 2 * h + e, first : first + P], ident_f32[:])
+                    copy_shared(out=grouped_words[:, g, h, :, :, :], in_=planes[:].rearrange("p e u m -> p m e u"))
+
+        def quantise_exemplars(grouped, c):
+            chunk = slice(c * K_PASS, (c + 1) * K_PASS)
             for g in range(F_PASSES):
                 nc.vector.quantize_mx(
-                    out=codes[:, g, cols].bitcast(FP8X4), scales=scales[:, g, cols], in_=grouped[:, g, :]
+                    out=x_codes[:, g, chunk].bitcast(FP8X4), scales=x_scales[:, g, chunk], in_=grouped[:, g, :]
                 )
+
+        prepared = []
+
+        def prepare_next():
+            i = len(prepared)
+            if i > 0:
+                grouped, kind, index = prepared[i - 1]
+                if kind == "probes":
+                    quantise_probes(grouped, index)
+                elif kind == "exemplars":
+                    quantise_exemplars(grouped, index)
+            if i >= E_BLOCK:
+                prepared.append((None, "nothing", 0))
+                return
+            grouped = new_grouped()
+            raw = take_block(i)
+            if 1 <= i <= N_CHUNKS:
+                transpose_exemplars(raw, grouped)
+                prepared.append((grouped, "exemplars", i - 1))
+            else:
+                piece = 0 if i == 0 else i - N_CHUNKS
+                for r in range(F_PIECES[piece][1]):
+                    transpose_probe_tile(raw, grouped, F_PIECES[piece][1], r, copy_shared)
+                prepared.append((grouped, "probes", piece))
 
         def group_class_vectors(raw, e_grouped, i):
             chunks = slice(i * N_CHUNKS // E_PIECES, (i + 1) * N_CHUNKS // E_PIECES)
             e_raw = raw[:].rearrange("p (g t c) -> p g c t", g=N_CHUNKS, t=PACK)
-            nc.vector.tensor_copy(out=e_grouped[:, chunks, :, :], in_=e_raw[:, chunks, :, :])
+            nc.gpsimd.tensor_scalar(
+                out=e_grouped[:, chunks, :, :], in0=e_raw[:, chunks, :, :], scalar1=1.0, scalar2=0.0, op0=ALU.mult, op1=ALU.add
+            )
 
         s_banks = {}
         s_squares = {}
         a_tiles = {}
         abs_sums = {}
         inv_sums = {}
-        inv_rows = {}
+        a_norm = {}
         a_banks = {}
         a_grouped = {}
         a_mx = {}
         echoes = {}
+        row_sums, inv_raws, echo_banks, d_banks = {}, {}, {}, {}
 
         def similarities(j, c):
             probes = slice(j * P, (j + 1) * P)
@@ -179,32 +239,61 @@ def tile_minerva_old_pb_kernel(tc, f_unit, exf_unit, ex_class_reps, class_reps, 
             chunk = slice(c * K_PASS, (c + 1) * K_PASS)
             nc.vector.tensor_tensor(out=a_tiles[j][:, chunk], in0=s_squares[j, c][:], in1=s_banks[j, c][:], op=ALU.mult)
 
+        SUMS = STEPS_PER_TILE + 1
+
         def sum_magnitudes(step):
             j, i = divmod(step, STEPS_PER_TILE)
             if i == 0:
-                abs_sums[j] = small.tile([P, STEPS_PER_TILE + 1], F32, name="abs_sums", tag="abs_sums")
-            chunks = slice(i * RUN * K_PASS, (i + 1) * RUN * K_PASS)
-            magnitudes = work.tile([P, RUN * K_PASS], BF16, tag="magnitudes")
+                abs_sums[j] = small.tile([P, SUMS], F32, name="abs_sums", tag="abs_sums")
+            units = RUN if i < STEPS_PER_TILE - 1 else RUN - 1
+            cols = slice(i * RUN * K_PASS, (i * RUN + units) * K_PASS)
+            magnitudes = junk.tile([P, RUN * K_PASS], BF16, tag="magnitudes")
             nc.scalar.activation(
-                out=magnitudes[:], in_=a_tiles[j][:, chunks], func=ACT.Abs, accum_out=abs_sums[j][:, i : i + 1]
+                out=magnitudes[:, 0 : units * K_PASS], in_=a_tiles[j][:, cols], func=ACT.Abs, accum_out=abs_sums[j][:, i : i + 1]
             )
 
-        def transpose_group(j, g):
-            a_t = psum_t.tile([P, PACK, P], F32, tag="t")
-            for t in range(PACK):
-                first = g * K_PASS + t * P
-                nc.tensor.transpose(a_t[:, t, :], a_tiles[j][:, first : first + P], ident_f32[:])
-            a_banks[j, g] = a_t
+        def sum_last_magnitudes(j):
+            nc.vector.tensor_reduce(
+                out=abs_sums[j][:, SUMS - 1 : SUMS], in_=a_tiles[j][:, N - K_PASS : N], axis=AXIS.X, op=ALU.add,
+                apply_absolute_value=True,
+            )
 
-        def normalise_group(j, g):
-            if g == 0:
+        def normalise(step, engine):
+            j, i = divmod(step, STEPS_PER_TILE)
+            if i == 0:
+                a_norm[j] = stage.tile([P, N], BF16, name="a_norm", tag="a_norm")
+            cols = slice(i * RUN * K_PASS, (i + 1) * RUN * K_PASS)
+            if engine == "scalar":
+                nc.scalar.activation(out=a_norm[j][:, cols], in_=a_tiles[j][:, cols], func=ACT.Copy, scale=inv_sums[j][:, 0:1])
+            elif engine == "gpsimd":
+                for u in range(RUN):
+                    part = slice((i * RUN + u) * K_PASS, (i * RUN + u + 1) * K_PASS)
+                    nc.gpsimd.tensor_scalar(
+                        out=a_norm[j][:, part], in0=a_tiles[j][:, part], scalar1=inv_sums[j][:, 0:1], scalar2=0.0,
+                        op0=ALU.mult, op1=ALU.add,
+                    )
+            else:
+                nc.vector.tensor_scalar(
+                    out=a_norm[j][:, cols], in0=a_tiles[j][:, cols], scalar1=inv_sums[j][:, 0:1], scalar2=None, op0=ALU.mult
+                )
+
+        def transpose_group(step):
+            j, i = divmod(step, STEPS_PER_TILE)
+            words = a_norm[j][:].bitcast(F32)
+            a_t = psum_t.tile([P, RUN, 2, P], F32, tag="t")
+            for g in range(RUN):
+                for h in range(2):
+                    first = ((i * RUN + g) * 2 + h) * P
+                    nc.tensor.transpose(a_t[:, g, h, :], words[:, first : first + P], ident_f32[:])
+            a_banks[step] = a_t
+
+        def copy_group(step, copy):
+            j, i = divmod(step, STEPS_PER_TILE)
+            if i == 0:
                 a_grouped[j] = stage.tile([P, N_CHUNKS, P, PACK], BF16, name="a_grouped", tag="a_grouped", align_bytes=64)
-            nc.vector.tensor_tensor(
-                out=a_grouped[j][:, g, :, :],
-                in0=a_banks[j, g][:].rearrange("p t b -> p b t"),
-                in1=inv_rows[j][:].unsqueeze(2).to_broadcast([P, P, PACK]),
-                op=ALU.mult,
-            )
+            grouped_words = a_grouped[j][:].rearrange("p g b t -> p (g b t)").bitcast(F32).rearrange("p (g b h) -> p g b h", g=N_CHUNKS, h=2)
+            chunks = slice(i * RUN, (i + 1) * RUN)
+            copy(out=grouped_words[:, chunks, :, :], in_=a_banks[step][:].rearrange("p g h b -> p g b h"))
 
         def quantise_half(j, h):
             if h == 0:
@@ -221,21 +310,76 @@ def tile_minerva_old_pb_kernel(tc, f_unit, exf_unit, ex_class_reps, class_reps, 
                 in_=a_grouped[j][:, chunks, :, :].rearrange("p g b t -> p (g b t)"),
             )
 
-        x_grouped = {}
+        def row_sum_of(j):
+            row_sums[j] = small.tile([P, 1], F32, name="row_sum", tag="row_sum")
+            nc.vector.tensor_reduce(out=row_sums[j][:], in_=abs_sums[j][:], axis=AXIS.X, op=ALU.add)
 
-        def prepare_exemplars(c):
-            if 0 < c <= N_CHUNKS:
-                quantise_rows(x_grouped[c - 1], x_codes, x_scales, slice((c - 1) * K_PASS, c * K_PASS))
-            if c < N_CHUNKS:
-                x_grouped[c] = transpose_rows(take_block(1 + c), SCALAR_ROW_TILES)
+        def invert(j):
+            inv_raws[j] = small.tile([P, 1], F32, name="inv_raw", tag="inv_raw")
+            nc.vector.reciprocal(out=inv_raws[j][:], in_=row_sums[j][:])
 
-        f_grouped = transpose_rows(take_block(0), SCALAR_ROW_TILES)
-        prepare_exemplars(0)
-        quantise_rows(f_grouped, f_codes, f_scales, slice(0, K_PASS))
-        for c in range(1, PREPARE_AHEAD):
-            prepare_exemplars(c)
+        def clamp(j):
+            inv_sums[j] = small.tile([P, 1], F32, name="inv_sum", tag="inv_sum")
+            nc.vector.tensor_scalar(out=inv_sums[j][:], in0=inv_raws[j][:], scalar1=1.0 / EPS, scalar2=None, op0=ALU.min)
 
-        cls_ps = psum_m.tile([P, P], BF16, tag="m")
+        def echo_matmuls(j):
+            a_codes, a_scales = a_mx[j]
+            if j < B_TILES - 1:
+                echo_banks[j] = psum_t.tile([P, P], F32, name="echo_ps", tag="t")
+            else:
+                echo_banks[j] = psum_s.tile([P, P], F32, name="echo_ps", tag="s")
+            for g in range(N_CHUNKS):
+                cols = slice(g * P, (g + 1) * P)
+                nc.tensor.matmul_mx(
+                    out=echo_banks[j][:],
+                    lhsT=e_codes[:, cols].bitcast(FP8X4),
+                    lhsT_scale=e_scales[:, cols],
+                    rhs=a_codes[:, cols].bitcast(FP8X4),
+                    rhs_scale=a_scales[:, cols],
+                    start=(g == 0),
+                    stop=(g == N_CHUNKS - 1),
+                )
+
+        def echo_out(j):
+            echo = small.tile([P, P], F32, tag="echo")
+            nc.scalar.copy(out=echo[:], in_=echo_banks[j][:])
+            echo_sq = small.tile([P, P], F32, tag="echo_sq")
+            nc.scalar.activation(out=echo_sq[:], in_=echo_banks[j][:], func=ACT.Square)
+            echoes[j] = (echo, echo_sq)
+
+        def distance_matmuls(j):
+            echo, echo_sq = echoes[j]
+            d_banks[j] = psum_t.tile([P, L_PAD], F32, name="d_ps", tag="t")
+            nc.tensor.matmul(out=d_banks[j][:], lhsT=echo_sq[:], rhs=ones[:, 0:L_PAD], start=True, stop=False)
+            nc.tensor.matmul(out=d_banks[j][:], lhsT=echo[:], rhs=cls_m2[:], start=False, stop=False)
+            nc.tensor.matmul(out=d_banks[j][:], lhsT=ones[:], rhs=cls_sq[:], start=False, stop=True)
+
+        def distance_out(j):
+            nc.scalar.activation(out=dist_sq[:, j, :], in_=d_banks[j][:, 0:L], func=ACT.Relu)
+
+        def roots(tiles):
+            nc.scalar.activation(out=dist[:, tiles, :], in_=dist_sq[:, tiles, :], func=ACT.Sqrt)
+            nc.vector.tensor_scalar(out=result[:, tiles, :], in0=dist[:, tiles, :], scalar1=-1.0, scalar2=None, op0=ALU.mult)
+
+        def quantise_piece(step):
+            j, i = divmod(step, STEPS_PER_TILE)
+            if i == 0:
+                a_mx[j] = (
+                    stage.tile([P, N_CHUNKS * P], U32, name="a_codes", tag="a_codes", align_bytes=64),
+                    stage.tile([P, N_CHUNKS * P], U8, name="a_scales", tag="a_scales", align_bytes=64),
+                )
+            a_codes, a_scales = a_mx[j]
+            words = slice(i * RUN * P, (i + 1) * RUN * P)
+            nc.vector.quantize_mx(
+                out=a_codes[:, words].bitcast(FP8X4),
+                scales=a_scales[:, words],
+                in_=a_grouped[j][:, i * RUN : (i + 1) * RUN, :, :].rearrange("p g b t -> p (g b t)"),
+            )
+
+        for i in range(1 + PREPARE_AHEAD):
+            prepare_next()
+
+        cls_ps = psum_t.tile([P, P], BF16, tag="t")
         nc.tensor.transpose(cls_ps[:], cls_pad[:], ident_bf16[:])
         cls_t = consts.tile([P, L_PAD], F32)
         nc.vector.tensor_copy(out=cls_t[:], in_=cls_ps[:, 0:L_PAD])
@@ -244,106 +388,105 @@ def tile_minerva_old_pb_kernel(tc, f_unit, exf_unit, ex_class_reps, class_reps, 
         cls_sq = consts.tile([P, L_PAD], F32)
         nc.vector.tensor_tensor(out=cls_sq[:], in0=cls_t[:], in1=cls_t[:], op=ALU.mult)
 
-        for step in range(STEPS + DIST_LAG + 1):
+        for step in range(STEPS):
             summed = tile_ending_at(step - SUM_LAG)
-            spread = tile_ending_at(step - SPREAD_LAG)
-            groups = units_of(step - GROUP_LAG)
 
-            if spread is not None:
-                inv_cols = small.tile([P, P], F32, tag="inv_cols")
-                nc.vector.tensor_scalar(
-                    out=inv_cols[:], in0=ones[:], scalar1=inv_sums[spread][:, 0:1], scalar2=1.0 / EPS,
-                    op0=ALU.mult, op1=ALU.min,
-                )
+            if step >= NORM_LAG:
+                normalise(step - NORM_LAG, "gpsimd")
+
+            if summed is not None:
+                sum_last_magnitudes(summed)
 
             for j, c in units_of(step):
                 similarities(j, c)
                 if j == 0:
-                    prepare_exemplars(c + PREPARE_AHEAD)
+                    prepare_next()
             for j, c in units_of(step):
                 cube(j, c)
-            if 0 <= step - QUANT_LAG < STEPS and (step - QUANT_LAG + 1) % HALF_STEPS == 0:
-                quantise_half(*divmod((step - QUANT_LAG) // HALF_STEPS, 2))
 
-            if 0 <= step - SUM_LAG < STEPS:
+            if step >= SUM_LAG:
                 sum_magnitudes(step - SUM_LAG)
-            if summed is not None:
-                sums_copy = small.tile([P, STEPS_PER_TILE], F32, tag="sums_copy")
-                nc.scalar.activation(
-                    out=sums_copy[:], in_=abs_sums[summed][:, 0:STEPS_PER_TILE], func=ACT.Copy,
-                    accum_out=abs_sums[summed][:, STEPS_PER_TILE : STEPS_PER_TILE + 1],
-                )
 
-            for j, g in groups:
-                transpose_group(j, g)
+            if step >= GROUP_LAG:
+                transpose_group(step - GROUP_LAG)
             r = step - F_STEP
             if r == 0:
-                f_raw = take_block(2 + N_CHUNKS)
-                f_grouped = grouped_pool.tile([P, F_PASSES, K_PASS * PACK], BF16, tag="grouped", align_bytes=64)
-            if 0 <= r < ROW_TILES:
-                transpose_row_tile(f_raw, f_grouped, r, True)
-            if spread is not None:
-                inv_ps = psum_m.tile([P, P], F32, tag="m")
-                nc.tensor.transpose(inv_ps[:], inv_cols[:], ident_f32[:])
+                f_raw = take_block(E_BLOCK + 1)
+                f_grouped = new_grouped()
+            if 0 <= r < F_PIECES[3][1]:
+                transpose_probe_tile(f_raw, f_grouped, F_PIECES[3][1], r, nc.scalar.copy)
 
-            for j, g in groups[:1]:
-                normalise_group(j, g)
             if summed is not None:
-                inv_sums[summed] = small.tile([P, 1], F32, name="inv_sum", tag="inv_sum")
-                nc.vector.reciprocal(
-                    out=inv_sums[summed][:], in_=abs_sums[summed][:, STEPS_PER_TILE : STEPS_PER_TILE + 1]
-                )
-            for j, g in groups[1:]:
-                normalise_group(j, g)
-            if spread is not None:
-                inv_rows[spread] = small.tile([P, P], F32, name="inv_rows", tag="inv_rows")
-                nc.scalar.copy(out=inv_rows[spread][:], in_=inv_ps[:])
+                row_sum_of(summed)
+            if step >= GROUP_LAG:
+                copy_group(step - GROUP_LAG, nc.vector.tensor_copy)
+            if summed is not None:
+                invert(summed)
+            if step >= QUANT_LAG and (step - QUANT_LAG + 1) % HALF_STEPS == 0:
+                quantise_half(*divmod((step - QUANT_LAG) // HALF_STEPS, 2))
+            if summed is not None:
+                clamp(summed)
 
-            i = step - E_STEP
-            if i == 0:
-                e_raw = take_block(1 + N_CHUNKS)
-                e_grouped = grouped_pool.tile([P, N_CHUNKS, C, PACK], BF16, tag="grouped", align_bytes=64)
-            if 0 <= i < E_PIECES:
-                group_class_vectors(e_raw, e_grouped, i)
-            if i == E_PIECES:
+            if step == E_STEP:
+                e_raw = take_block(E_BLOCK)
+                e_grouped = stage.tile([P, N_CHUNKS, C, PACK], BF16, name="e_grouped", tag="a_grouped", align_bytes=64)
+                for i in range(E_PIECES):
+                    group_class_vectors(e_raw, e_grouped, i)
+            if step == E_QUANT_STEP:
                 nc.vector.quantize_mx(
                     out=e_codes[:].bitcast(FP8X4), scales=e_scales[:], in_=e_grouped[:].rearrange("p g c t -> p (g c t)")
                 )
-            if step == F_STEP + ROW_TILES:
-                quantise_rows(f_grouped, f_codes, f_scales, slice(K_PASS, 2 * K_PASS))
+            if step == F_STEP + F_PIECES[3][1]:
+                quantise_probes(f_grouped, 3)
 
             j = tile_ending_at(step - ECHO_LAG)
             if j is not None:
-                a_codes, a_scales = a_mx[j]
-                echo_ps = psum_m.tile([P, P], F32, tag="m")
-                for g in range(N_CHUNKS):
-                    cols = slice(g * P, (g + 1) * P)
-                    nc.tensor.matmul_mx(
-                        out=echo_ps[:],
-                        lhsT=e_codes[:, cols].bitcast(FP8X4),
-                        lhsT_scale=e_scales[:, cols],
-                        rhs=a_codes[:, cols].bitcast(FP8X4),
-                        rhs_scale=a_scales[:, cols],
-                        start=(g == 0),
-                        stop=(g == N_CHUNKS - 1),
-                    )
-                echo = small.tile([P, P], F32, tag="echo")
-                nc.scalar.copy(out=echo[:], in_=echo_ps[:])
-                echo_sq = small.tile([P, P], F32, tag="echo_sq")
-                nc.scalar.activation(out=echo_sq[:], in_=echo_ps[:], func=ACT.Square)
-                echoes[j] = (echo, echo_sq)
-
+                echo_matmuls(j)
+                echo_out(j)
             j = tile_ending_at(step - DIST_LAG)
             if j is not None:
-                echo, echo_sq = echoes[j]
-                d_ps = psum_m.tile([P, L_PAD], F32, tag="m")
-                nc.tensor.matmul(out=d_ps[:], lhsT=echo_sq[:], rhs=ones[:, 0:L_PAD], start=True, stop=False)
-                nc.tensor.matmul(out=d_ps[:], lhsT=echo[:], rhs=cls_m2[:], start=False, stop=False)
-                nc.tensor.matmul(out=d_ps[:], lhsT=ones[:], rhs=cls_sq[:], start=False, stop=True)
-                nc.scalar.activation(out=dist_sq[:, j, :], in_=d_ps[:, 0:L], func=ACT.Relu)
+                distance_matmuls(j)
+                distance_out(j)
 
-        dist = keep.tile([P, B_TILES, L], F32)
-        nc.scalar.activation(out=dist[:], in_=dist_sq[:], func=ACT.Sqrt)
-        result = keep.tile([P, B_TILES, L], F32)
-        nc.vector.tensor_scalar(out=result[:], in0=dist[:], scalar1=-1.0, scalar2=None, op0=ALU.mult)
+        last = B_TILES - 1
+        first_left = STEPS - GROUP_LAG
+        normalise(STEPS - NORM_LAG, "gpsimd")
+        sum_last_magnitudes(last)
+        sum_magnitudes(STEPS - 1)
+        transpose_group(first_left)
+        echo_matmuls(last - 2)
+        copy_group(first_left, nc.scalar.copy)
+        row_sum_of(last)
+        invert(last)
+        clamp(last)
+        echo_out(last - 2)
+        for i in range(STEPS_PER_TILE - 1):
+            normalise(LAST_TILE_STEP + i, "vector")
+        normalise(STEPS - 1, "scalar")
+        transpose_group(first_left + 1)
+        distance_matmuls(last - 2)
+        for i in range(STEPS_PER_TILE):
+            transpose_group(LAST_TILE_STEP + i)
+        copy_group(first_left + 1, nc.scalar.copy)
+        distance_out(last - 2)
+        quantise_half(last - 1, 0)
+        copy_group(LAST_TILE_STEP, nc.scalar.copy)
+        quantise_half(last - 1, 1)
+        copy_group(LAST_TILE_STEP + 1, nc.scalar.copy)
+        quantise_piece(LAST_TILE_STEP)
+        copy_group(LAST_TILE_STEP + 2, nc.scalar.copy)
+        quantise_piece(LAST_TILE_STEP + 1)
+        copy_group(LAST_TILE_STEP + 3, nc.scalar.copy)
+        quantise_piece(LAST_TILE_STEP + 2)
+        echo_matmuls(last - 1)
+        echo_out(last - 1)
+        quantise_piece(LAST_TILE_STEP + 3)
+        distance_matmuls(last - 1)
+        distance_out(last - 1)
+        roots(slice(0, last))
+        echo_matmuls(last)
+        echo_out(last)
+        distance_matmuls(last)
+        distance_out(last)
+        roots(slice(last, B_TILES))
         nc.sync.dma_start(out=out.rearrange("(p j) l -> p j l", j=B_TILES), in_=result[:])

@@ -43,7 +43,7 @@ E_QUANT_STEP = E_STEP + 3
 F_STEP = 2 * STEPS_PER_TILE
 PREPARE_AHEAD = 3
 AHEAD = 3
-SCALAR_SHARE = (3, 4)
+SCALAR_SHARE = (2, 3)
 
 FLOPS = 2 * B * N * F + 2 * B * N * C
 

@@ -40,7 +40,7 @@ F_PIECES = ((0, 1), (1, 1), (2, 2), (4, 4))
 E_STEP = STEPS_PER_TILE - 1
 E_PIECES = 4
 E_QUANT_STEP = E_STEP + 3
-F_STEP = 2 * STEPS_PER_TILE
+F_STEP = STEPS_PER_TILE + 1
 PREPARE_AHEAD = 3
 AHEAD = 3
 SCALAR_SHARE = (2, 3)

@@ -212,7 +212,7 @@ def tile_minerva_old_pb_kernel(tc, f_unit, exf_unit, ex_class_reps, class_reps, 
         a_grouped = {}
         a_mx = {}
         echoes = {}
-        row_sums, inv_raws, echo_banks, d_banks = {}, {}, {}, {}
+        row_sums, inv_raws, echo_banks, d_banks, early_sums, late_sums = {}, {}, {}, {}, {}, {}
 
         def similarities(j, c):
             probes = slice(j * P, (j + 1) * P)
@@ -314,6 +314,26 @@ def tile_minerva_old_pb_kernel(tc, f_unit, exf_unit, ex_class_reps, class_reps, 
             row_sums[j] = small.tile([P, 1], F32, name="row_sum", tag="row_sum")
             nc.vector.tensor_reduce(out=row_sums[j][:], in_=abs_sums[j][:], axis=AXIS.X, op=ALU.add)
 
+        def row_sum_but_last(j):
+            early_sums[j] = small.tile([P, 1], F32, name="early_sum", tag="early_sum")
+            nc.vector.tensor_reduce(out=early_sums[j][:], in_=abs_sums[j][:, 0 : SUMS - 2], axis=AXIS.X, op=ALU.add)
+
+        def add_vector_sum(j):
+            late_sums[j] = small.tile([P, 1], F32, name="late_sum", tag="late_sum")
+            nc.vector.tensor_scalar(
+                out=late_sums[j][:], in0=early_sums[j][:], scalar1=abs_sums[j][:, SUMS - 1 : SUMS], scalar2=None, op0=ALU.add
+            )
+
+        def add_scalar_sum(j):
+            row_sums[j] = small.tile([P, 1], F32, name="row_sum", tag="row_sum")
+            nc.vector.tensor_scalar(
+                out=row_sums[j][:], in0=late_sums[j][:], scalar1=abs_sums[j][:, SUMS - 2 : SUMS - 1], scalar2=EPS, op0=ALU.add, op1=ALU.max
+            )
+
+        def invert_last(j):
+            inv_sums[j] = small.tile([P, 1], F32, name="inv_sum", tag="inv_sum")
+            nc.vector.reciprocal(out=inv_sums[j][:], in_=row_sums[j][:])
+
         def invert(j):
             inv_raws[j] = small.tile([P, 1], F32, name="inv_raw", tag="inv_raw")
             nc.vector.reciprocal(out=inv_raws[j][:], in_=row_sums[j][:])
@@ -324,7 +344,7 @@ def tile_minerva_old_pb_kernel(tc, f_unit, exf_unit, ex_class_reps, class_reps, 
 
         def echo_matmuls(j):
             a_codes, a_scales = a_mx[j]
-            if j < B_TILES - 1:
+            if j < B_TILES - 2:
                 echo_banks[j] = psum_t.tile([P, P], F32, name="echo_ps", tag="t")
             else:
                 echo_banks[j] = psum_s.tile([P, P], F32, name="echo_ps", tag="s")
@@ -340,26 +360,28 @@ def tile_minerva_old_pb_kernel(tc, f_unit, exf_unit, ex_class_reps, class_reps, 
                     stop=(g == N_CHUNKS - 1),
                 )
 
-        def echo_out(j):
+        def echo_out(j, copy):
             echo = small.tile([P, P], F32, tag="echo")
-            nc.scalar.copy(out=echo[:], in_=echo_banks[j][:])
+            copy(out=echo[:], in_=echo_banks[j][:])
             echo_sq = small.tile([P, P], F32, tag="echo_sq")
             nc.scalar.activation(out=echo_sq[:], in_=echo_banks[j][:], func=ACT.Square)
             echoes[j] = (echo, echo_sq)
 
-        def distance_matmuls(j):
-            echo, echo_sq = echoes[j]
+        def class_terms(j):
             d_banks[j] = psum_t.tile([P, L_PAD], F32, name="d_ps", tag="t")
-            nc.tensor.matmul(out=d_banks[j][:], lhsT=echo_sq[:], rhs=ones[:, 0:L_PAD], start=True, stop=False)
+            nc.tensor.matmul(out=d_banks[j][:], lhsT=ones[:], rhs=cls_sq[:], start=True, stop=False)
+
+        def echo_terms(j):
+            echo, echo_sq = echoes[j]
             nc.tensor.matmul(out=d_banks[j][:], lhsT=echo[:], rhs=cls_m2[:], start=False, stop=False)
-            nc.tensor.matmul(out=d_banks[j][:], lhsT=ones[:], rhs=cls_sq[:], start=False, stop=True)
+            nc.tensor.matmul(out=d_banks[j][:], lhsT=echo_sq[:], rhs=ones[:, 0:L_PAD], start=False, stop=True)
 
         def distance_out(j):
             nc.scalar.activation(out=dist_sq[:, j, :], in_=d_banks[j][:, 0:L], func=ACT.Relu)
 
         def roots(tiles):
             nc.scalar.activation(out=dist[:, tiles, :], in_=dist_sq[:, tiles, :], func=ACT.Sqrt)
-            nc.vector.tensor_scalar(out=result[:, tiles, :], in0=dist[:, tiles, :], scalar1=-1.0, scalar2=None, op0=ALU.mult)
+            nc.scalar.mul(result[:, tiles, :], dist[:, tiles, :], -1.0)
 
         def quantise_piece(step):
             j, i = divmod(step, STEPS_PER_TILE)
@@ -403,6 +425,9 @@ def tile_minerva_old_pb_kernel(tc, f_unit, exf_unit, ex_class_reps, class_reps, 
                     prepare_next()
             for j, c in units_of(step):
                 cube(j, c)
+            if step == STEPS - 1:
+                quantise_piece(STEPS - GROUP_LAG - 2)
+                sum_last_magnitudes(B_TILES - 1)
 
             if step >= SUM_LAG:
                 sum_magnitudes(step - SUM_LAG)
@@ -418,7 +443,7 @@ def tile_minerva_old_pb_kernel(tc, f_unit, exf_unit, ex_class_reps, class_reps, 
 
             if summed is not None:
                 row_sum_of(summed)
-            if step >= GROUP_LAG:
+            if GROUP_LAG <= step < STEPS - 1:
                 copy_group(step - GROUP_LAG, nc.vector.tensor_copy)
             if summed is not None:
                 invert(summed)
@@ -442,51 +467,56 @@ def tile_minerva_old_pb_kernel(tc, f_unit, exf_unit, ex_class_reps, class_reps, 
             j = tile_ending_at(step - ECHO_LAG)
             if j is not None:
                 echo_matmuls(j)
-                echo_out(j)
+                echo_out(j, nc.scalar.copy)
             j = tile_ending_at(step - DIST_LAG)
             if j is not None:
-                distance_matmuls(j)
+                class_terms(j)
+                echo_terms(j)
                 distance_out(j)
 
         last = B_TILES - 1
         first_left = STEPS - GROUP_LAG
         normalise(STEPS - NORM_LAG, "gpsimd")
-        sum_last_magnitudes(last)
         sum_magnitudes(STEPS - 1)
         transpose_group(first_left)
         echo_matmuls(last - 2)
-        copy_group(first_left, nc.scalar.copy)
-        row_sum_of(last)
-        invert(last)
-        clamp(last)
-        echo_out(last - 2)
-        for i in range(STEPS_PER_TILE - 1):
-            normalise(LAST_TILE_STEP + i, "vector")
-        normalise(STEPS - 1, "scalar")
         transpose_group(first_left + 1)
-        distance_matmuls(last - 2)
-        for i in range(STEPS_PER_TILE):
-            transpose_group(LAST_TILE_STEP + i)
+        row_sum_but_last(last)
+        copy_group(first_left - 1, nc.scalar.copy)
+        add_vector_sum(last)
+        echo_out(last - 2, nc.scalar.copy)
+        class_terms(last - 2)
+        echo_terms(last - 2)
+        copy_group(first_left, nc.scalar.copy)
+        add_scalar_sum(last)
         copy_group(first_left + 1, nc.scalar.copy)
         distance_out(last - 2)
-        quantise_half(last - 1, 0)
+        invert_last(last)
+        quantise_piece(first_left - 1)
+        for i in range(STEPS_PER_TILE):
+            normalise(LAST_TILE_STEP + i, "vector")
+        for i in range(STEPS_PER_TILE):
+            transpose_group(LAST_TILE_STEP + i)
         copy_group(LAST_TILE_STEP, nc.scalar.copy)
-        quantise_half(last - 1, 1)
+        class_terms(last - 1)
         copy_group(LAST_TILE_STEP + 1, nc.scalar.copy)
-        quantise_piece(LAST_TILE_STEP)
+        class_terms(last)
+        quantise_piece(first_left)
         copy_group(LAST_TILE_STEP + 2, nc.scalar.copy)
-        quantise_piece(LAST_TILE_STEP + 1)
-        copy_group(LAST_TILE_STEP + 3, nc.scalar.copy)
-        quantise_piece(LAST_TILE_STEP + 2)
+        quantise_piece(first_left + 1)
         echo_matmuls(last - 1)
-        echo_out(last - 1)
+        quantise_piece(LAST_TILE_STEP)
+        copy_group(LAST_TILE_STEP + 3, nc.scalar.copy)
+        roots(slice(0, last - 1))
+        quantise_piece(LAST_TILE_STEP + 1)
+        quantise_piece(LAST_TILE_STEP + 2)
         quantise_piece(LAST_TILE_STEP + 3)
-        distance_matmuls(last - 1)
-        distance_out(last - 1)
-        roots(slice(0, last))
+        echo_out(last - 1, nc.vector.tensor_copy)
         echo_matmuls(last)
-        echo_out(last)
-        distance_matmuls(last)
+        echo_out(last, nc.vector.tensor_copy)
+        echo_terms(last - 1)
+        echo_terms(last)
+        distance_out(last - 1)
         distance_out(last)
-        roots(slice(last, B_TILES))
+        roots(slice(last - 1, B_TILES))
         nc.sync.dma_start(out=out.rearrange("(p j) l -> p j l", j=B_TILES), in_=result[:])

@@ -40,7 +40,7 @@ F_PIECES = ((0, 1), (1, 1), (2, 2), (4, 4))
 E_STEP = STEPS_PER_TILE - 1
 E_PIECES = 4
 E_QUANT_STEP = E_STEP + 3
-F_STEP = STEPS_PER_TILE + 1
+F_STEP = 2 * STEPS_PER_TILE - 1
 PREPARE_AHEAD = 3
 AHEAD = 3
 SCALAR_SHARE = (2, 3)
@@ -52,6 +52,13 @@ def units_of(step):
     if step < 0 or step >= STEPS:
         return []
     return [divmod(unit, N_CHUNKS) for unit in range(step * RUN, (step + 1) * RUN)]
+
+
+def groups_of(step):
+    group = step - GROUP_LAG
+    if group < 0 or group % STEPS_PER_TILE == 0:
+        return []
+    return [group - 1, group] if group % STEPS_PER_TILE == 1 else [group]
 
 
 def tile_ending_at(step):
@@ -266,12 +273,9 @@ def tile_minerva_old_pb_kernel(tc, f_unit, exf_unit, ex_class_reps, class_reps, 
             if engine == "scalar":
                 nc.scalar.activation(out=a_norm[j][:, cols], in_=a_tiles[j][:, cols], func=ACT.Copy, scale=inv_sums[j][:, 0:1])
             elif engine == "gpsimd":
-                for u in range(RUN):
-                    part = slice((i * RUN + u) * K_PASS, (i * RUN + u + 1) * K_PASS)
-                    nc.gpsimd.tensor_scalar(
-                        out=a_norm[j][:, part], in0=a_tiles[j][:, part], scalar1=inv_sums[j][:, 0:1], scalar2=0.0,
-                        op0=ALU.mult, op1=ALU.add,
-                    )
+                nc.gpsimd.tensor_scalar(
+                    out=a_norm[j][:, cols], in0=a_tiles[j][:, cols], scalar1=inv_sums[j][:, 0:1], scalar2=0.0, op0=ALU.mult, op1=ALU.add
+                )
             else:
                 nc.vector.tensor_scalar(
                     out=a_norm[j][:, cols], in0=a_tiles[j][:, cols], scalar1=inv_sums[j][:, 0:1], scalar2=None, op0=ALU.mult
@@ -426,14 +430,13 @@ def tile_minerva_old_pb_kernel(tc, f_unit, exf_unit, ex_class_reps, class_reps, 
             for j, c in units_of(step):
                 cube(j, c)
             if step == STEPS - 1:
-                quantise_piece(STEPS - GROUP_LAG - 2)
                 sum_last_magnitudes(B_TILES - 1)
 
             if step >= SUM_LAG:
                 sum_magnitudes(step - SUM_LAG)
 
-            if step >= GROUP_LAG:
-                transpose_group(step - GROUP_LAG)
+            for group in groups_of(step):
+                transpose_group(group)
             r = step - F_STEP
             if r == 0:
                 f_raw = take_block(E_BLOCK + 1)
@@ -443,8 +446,9 @@ def tile_minerva_old_pb_kernel(tc, f_unit, exf_unit, ex_class_reps, class_reps, 
 
             if summed is not None:
                 row_sum_of(summed)
-            if GROUP_LAG <= step < STEPS - 1:
-                copy_group(step - GROUP_LAG, nc.vector.tensor_copy)
+            if step < STEPS - 1:
+                for group in groups_of(step):
+                    copy_group(group, nc.vector.tensor_copy)
             if summed is not None:
                 invert(summed)
             if step >= QUANT_LAG and (step - QUANT_LAG + 1) % HALF_STEPS == 0:
@@ -482,17 +486,18 @@ def tile_minerva_old_pb_kernel(tc, f_unit, exf_unit, ex_class_reps, class_reps, 
         echo_matmuls(last - 2)
         transpose_group(first_left + 1)
         row_sum_but_last(last)
-        copy_group(first_left - 1, nc.scalar.copy)
+        copy_group(first_left - 2, nc.scalar.copy)
         add_vector_sum(last)
         echo_out(last - 2, nc.scalar.copy)
         class_terms(last - 2)
         echo_terms(last - 2)
-        copy_group(first_left, nc.scalar.copy)
+        copy_group(first_left - 1, nc.scalar.copy)
         add_scalar_sum(last)
+        copy_group(first_left, nc.scalar.copy)
         copy_group(first_left + 1, nc.scalar.copy)
         distance_out(last - 2)
         invert_last(last)
-        quantise_piece(first_left - 1)
+        quantise_piece(first_left - 2)
         for i in range(STEPS_PER_TILE):
             normalise(LAST_TILE_STEP + i, "vector")
         for i in range(STEPS_PER_TILE):
@@ -501,6 +506,7 @@ def tile_minerva_old_pb_kernel(tc, f_unit, exf_unit, ex_class_reps, class_reps, 
         class_terms(last - 1)
         copy_group(LAST_TILE_STEP + 1, nc.scalar.copy)
         class_terms(last)
+        quantise_piece(first_left - 1)
         quantise_piece(first_left)
         copy_group(LAST_TILE_STEP + 2, nc.scalar.copy)
         quantise_piece(first_left + 1)

from contextlib import ExitStack

import concourse.mybir as mybir
from concourse.masks import make_identity

F32 = mybir.dt.float32
BF16 = mybir.dt.bfloat16
U32 = mybir.dt.uint32
U8 = mybir.dt.uint8
FP8X4 = mybir.dt.float8_e4m3fn_x4
ACT = mybir.ActivationFunctionType
ALU = mybir.AluOpType
AXIS = mybir.AxisListType

P = 128
PACK = 4
K_PASS = P * PACK

B, N, F, C, L = 1024, 4096, 1024, 128, 28
EPS = 1e-12

B_TILES = B // P
N_CHUNKS = N // K_PASS
F_PASSES = F // K_PASS
ROW_TILES = K_PASS // P
L_PAD = 32

RUN = 2
STEPS_PER_TILE = N_CHUNKS // RUN
STEPS = B_TILES * STEPS_PER_TILE
LAST_TILE_STEP = STEPS - STEPS_PER_TILE
HALF_STEPS = STEPS_PER_TILE // 2
SUM_LAG = 1
NORM_LAG = STEPS_PER_TILE + SUM_LAG
GROUP_LAG = NORM_LAG + 1
QUANT_LAG = GROUP_LAG + 1
ECHO_LAG = GROUP_LAG + 3
DIST_LAG = ECHO_LAG + 1
F_PIECES = ((0, 1), (1, 1), (2, 2), (4, 4))
E_STEP = STEPS_PER_TILE - 1
E_PIECES = 4
E_QUANT_STEP = E_STEP + 3
F_STEP = 2 * STEPS_PER_TILE - 1
PREPARE_AHEAD = 3
AHEAD = 3
SCALAR_SHARE = (2, 3)

FLOPS = 2 * B * N * F + 2 * B * N * C


def units_of(step):
    if step < 0 or step >= STEPS:
        return []
    return [divmod(unit, N_CHUNKS) for unit in range(step * RUN, (step + 1) * RUN)]


def groups_of(step):
    group = step - GROUP_LAG
    if group < 0 or group % STEPS_PER_TILE == 0:
        return []
    return [group - 1, group] if group % STEPS_PER_TILE == 1 else [group]


def tile_ending_at(step):
    if 0 <= step < STEPS and (step + 1) % STEPS_PER_TILE == 0:
        return step // STEPS_PER_TILE
    return None


def tile_minerva_old_pb_kernel(tc, f_unit, exf_unit, ex_class_reps, class_reps, out):
    nc = tc.nc
    with ExitStack() as stack:
        consts = stack.enter_context(tc.tile_pool(name="consts", bufs=1))
        keep = stack.enter_context(tc.tile_pool(name="keep", bufs=1))
        raw_pool = stack.enter_context(tc.tile_pool(name="raw", bufs=AHEAD + 1))
        stage = stack.enter_context(tc.tile_pool(name="stage", bufs=2))
        grouped_pool = stack.enter_context(tc.tile_pool(name="grouped", bufs=3))
        a_pool = stack.enter_context(tc.tile_pool(name="a", bufs=3))
        work = stack.enter_context(tc.tile_pool(name="work", bufs=4))
        junk = stack.enter_context(tc.tile_pool(name="junk", bufs=2))
        small = stack.enter_context(tc.tile_pool(name="small", bufs=2))
        psum_s = stack.enter_context(tc.psum_pool(name="psum_s", bufs=4))
        psum_t = stack.enter_context(tc.psum_pool(name="psum_t", bufs=4))
        stack.enter_context(tc.manual_schedule())

        f_rows = f_unit.rearrange("(p j) k -> p j k", j=B_TILES)
        f_blocks = [f_rows[:, first : first + tiles, :] for first, tiles in F_PIECES]
        x_blocks = [
            exf_unit[c * K_PASS : (c + 1) * K_PASS, :].rearrange("(p t) k -> p t k", t=PACK) for c in range(N_CHUNKS)
        ]
        e_block = ex_class_reps.rearrange("(g p t) c -> p g (t c)", p=P, t=PACK)
        blocks = f_blocks[0:1] + x_blocks + f_blocks[1:3] + [e_block] + f_blocks[3:4]
        E_BLOCK = len(blocks) - 2
        raw_tiles = {}

        def load_block(i):
            raw_tiles[i] = raw_pool.tile([P, ROW_TILES * F], BF16, name="raw", tag="raw")
            rows, width = blocks[i].shape[1], blocks[i].shape[2]
            nc.sync.dma_start(out=raw_tiles[i][:, 0 : rows * width].rearrange("p (r x) -> p r x", r=rows), in_=blocks[i])

        def take_block(i):
            if i + AHEAD < len(blocks):
                load_block(i + AHEAD)
            return raw_tiles[i]

        for i in range(AHEAD):
            load_block(i)
        cls_pad = consts.tile([P, C], BF16)
        nc.vector.memset(cls_pad[:], 0.0)
        nc.sync.dma_start(out=cls_pad[0:L, :], in_=class_reps)

        ident_f32 = consts.tile([P, P], F32)
        make_identity(nc, ident_f32[:])
        ident_bf16 = consts.tile([P, P], BF16)
        make_identity(nc, ident_bf16[:])
        ones = consts.tile([P, P], F32)
        nc.vector.memset(ones[:], 1.0)
        warm = consts.tile([P, 1], F32)
        nc.scalar.activation(out=warm[:], in_=ones[:, 0:1], func=ACT.Sqrt)

        f_codes = keep.tile([P, F_PASSES, B], U32, align_bytes=64)
        f_scales = keep.tile([P, F_PASSES, B], U8, align_bytes=64)
        x_codes = keep.tile([P, F_PASSES, N], U32, align_bytes=64)
        x_scales = keep.tile([P, F_PASSES, N], U8, align_bytes=64)
        e_codes = keep.tile([P, N_CHUNKS * C], U32, align_bytes=64)
        e_scales = keep.tile([P, N_CHUNKS * C], U8, align_bytes=64)
        dist_sq = keep.tile([P, B_TILES, L], F32)
        dist = keep.tile([P, B_TILES, L], F32)
        result = keep.tile([P, B_TILES, L], F32)

        banks_copied = [0]

        def copy_shared(out, in_):
            on_scalar = banks_copied[0] * SCALAR_SHARE[0] % SCALAR_SHARE[1] < SCALAR_SHARE[0]
            banks_copied[0] += 1
            if on_scalar:
                nc.scalar.copy(out=out, in_=in_)
            else:
                nc.vector.tensor_copy(out=out, in_=in_)

        def new_grouped():
            return grouped_pool.tile([P, F_PASSES, K_PASS * PACK], BF16, name="grouped", tag="grouped", align_bytes=64)

        def transpose_probe_tile(raw, grouped, tiles, r, copy):
            words = raw[:].bitcast(F32).rearrange("p (r w) -> p r w", r=ROW_TILES)
            grouped_words = grouped[:].bitcast(F32)[:, :, 0 : tiles * P * 2].rearrange("p g (r m u) -> p g r m u", r=tiles, u=2)
            planes = psum_t.tile([P, F_PASSES, 2, P], F32, tag="t")
            for g in range(F_PASSES):
                for u in range(2):
                    first = (2 * g + u) * P
                    nc.tensor.transpose(planes[:, g, u, :], words[:, r, first : first + P], ident_f32[:])
            copy(out=grouped_words[:, :, r, :, :], in_=planes[:].rearrange("p g u m -> p g m u"))

        def quantise_probes(grouped, piece):
            first, tiles = F_PIECES[piece]
            for g in range(F_PASSES):
                cols = slice(first * P, (first + tiles) * P)
                nc.vector.quantize_mx(
                    out=f_codes[:, g, cols].bitcast(FP8X4), scales=f_scales[:, g, cols], in_=grouped[:, g, 0 : tiles * K_PASS]
                )

        def transpose_exemplars(raw, grouped):
            words = raw[:].bitcast(F32).rearrange("p (r w) -> p r w", r=ROW_TILES)
            grouped_words = grouped[:].bitcast(F32).rearrange("p g (h m e u) -> p g h m e u", h=2, e=2, u=2)
            for g in range(F_PASSES):
                for h in range(2):
                    planes = psum_t.tile([P, 2, 2, P], F32, tag="t")
                    for e in range(2):
                        for u in range(2):
                            first = (2 * g + u) * P
                            nc.tensor.transpose(planes[:, e, u, :], words[:, 2 * h + e, first : first + P], ident_f32[:])
                    copy_shared(out=grouped_words[:, g, h, :, :, :], in_=planes[:].rearrange("p e u m -> p m e u"))

        def quantise_exemplars(grouped, c):
            chunk = slice(c * K_PASS, (c + 1) * K_PASS)
            for g in range(F_PASSES):
                nc.vector.quantize_mx(
                    out=x_codes[:, g, chunk].bitcast(FP8X4), scales=x_scales[:, g, chunk], in_=grouped[:, g, :]
                )

        prepared = []

        def prepare_next():
            i = len(prepared)
            if i > 0:
                grouped, kind, index = prepared[i - 1]
                if kind == "probes":
                    quantise_probes(grouped, index)
                elif kind == "exemplars":
                    quantise_exemplars(grouped, index)
            if i >= E_BLOCK:
                prepared.append((None, "nothing", 0))
                return
            grouped = new_grouped()
            raw = take_block(i)
            if 1 <= i <= N_CHUNKS:
                transpose_exemplars(raw, grouped)
                prepared.append((grouped, "exemplars", i - 1))
            else:
                piece = 0 if i == 0 else i - N_CHUNKS
                for r in range(F_PIECES[piece][1]):
                    transpose_probe_tile(raw, grouped, F_PIECES[piece][1], r, copy_shared)
                prepared.append((grouped, "probes", piece))

        def group_class_vectors(raw, e_grouped, i):
            chunks = slice(i * N_CHUNKS // E_PIECES, (i + 1) * N_CHUNKS // E_PIECES)
            e_raw = raw[:].rearrange("p (g t c) -> p g c t", g=N_CHUNKS, t=PACK)
            nc.gpsimd.tensor_scalar(
                out=e_grouped[:, chunks, :, :], in0=e_raw[:, chunks, :, :], scalar1=1.0, scalar2=0.0, op0=ALU.mult, op1=ALU.add
            )

        s_banks = {}
        s_squares = {}
        a_tiles = {}
        abs_sums = {}
        inv_sums = {}
        a_norm = {}
        a_banks = {}
        a_grouped = {}
        a_mx = {}
        echoes = {}
        row_sums, inv_raws, echo_banks, d_banks, early_sums, late_sums = {}, {}, {}, {}, {}, {}

        def similarities(j, c):
            probes = slice(j * P, (j + 1) * P)
            chunk = slice(c * K_PASS, (c + 1) * K_PASS)
            s_ps = psum_s.tile([P, K_PASS], F32, tag="s")
            for g in range(F_PASSES):
                nc.tensor.matmul_mx(
                    out=s_ps[:],
                    lhsT=f_codes[:, g, probes].bitcast(FP8X4),
                    lhsT_scale=f_scales[:, g, probes],
                    rhs=x_codes[:, g, chunk].bitcast(FP8X4),
                    rhs_scale=x_scales[:, g, chunk],
                    start=(g == 0),
                    stop=(g == F_PASSES - 1),
                )
            s_sq = work.tile([P, K_PASS], F32, tag="s_sq")
            nc.scalar.activation(out=s_sq[:], in_=s_ps[:], func=ACT.Square)
            s_banks[j, c] = s_ps
            s_squares[j, c] = s_sq

        def cube(j, c):
            if c == 0:
                a_tiles[j] = a_pool.tile([P, N], F32, name="a_rows", tag="a")
            chunk = slice(c * K_PASS, (c + 1) * K_PASS)
            nc.vector.tensor_tensor(out=a_tiles[j][:, chunk], in0=s_squares[j, c][:], in1=s_banks[j, c][:], op=ALU.mult)

        SUMS = STEPS_PER_TILE + 1

        def sum_magnitudes(step):
            j, i = divmod(step, STEPS_PER_TILE)
            if i == 0:
                abs_sums[j] = small.tile([P, SUMS], F32, name="abs_sums", tag="abs_sums")
            units = RUN if i < STEPS_PER_TILE - 1 else RUN - 1
            cols = slice(i * RUN * K_PASS, (i * RUN + units) * K_PASS)
            magnitudes = junk.tile([P, RUN * K_PASS], BF16, tag="magnitudes")
            nc.scalar.activation(
                out=magnitudes[:, 0 : units * K_PASS], in_=a_tiles[j][:, cols], func=ACT.Abs, accum_out=abs_sums[j][:, i : i + 1]
            )

        def sum_last_magnitudes(j):
            nc.vector.tensor_reduce(
                out=abs_sums[j][:, SUMS - 1 : SUMS], in_=a_tiles[j][:, N - K_PASS : N], axis=AXIS.X, op=ALU.add,
                apply_absolute_value=True,
            )

        def normalise(step, engine):
            j, i = divmod(step, STEPS_PER_TILE)
            if i == 0:
                a_norm[j] = stage.tile([P, N], BF16, name="a_norm", tag="a_norm")
            cols = slice(i * RUN * K_PASS, (i + 1) * RUN * K_PASS)
            if engine == "scalar":
                nc.scalar.activation(out=a_norm[j][:, cols], in_=a_tiles[j][:, cols], func=ACT.Copy, scale=inv_sums[j][:, 0:1])
            elif engine == "gpsimd":
                nc.gpsimd.tensor_scalar(
                    out=a_norm[j][:, cols], in0=a_tiles[j][:, cols], scalar1=inv_sums[j][:, 0:1], scalar2=0.0, op0=ALU.mult, op1=ALU.add
                )
            else:
                nc.vector.tensor_scalar(
                    out=a_norm[j][:, cols], in0=a_tiles[j][:, cols], scalar1=inv_sums[j][:, 0:1], scalar2=None, op0=ALU.mult
                )

        def transpose_group(step):
            j, i = divmod(step, STEPS_PER_TILE)
            words = a_norm[j][:].bitcast(F32)
            a_t = psum_t.tile([P, RUN, 2, P], F32, tag="t")
            for g in range(RUN):
                for h in range(2):
                    first = ((i * RUN + g) * 2 + h) * P
                    nc.tensor.transpose(a_t[:, g, h, :], words[:, first : first + P], ident_f32[:])
            a_banks[step] = a_t

        def copy_group(step, copy):
            j, i = divmod(step, STEPS_PER_TILE)
            if i == 0:
                a_grouped[j] = stage.tile([P, N_CHUNKS, P, PACK], BF16, name="a_grouped", tag="a_grouped", align_bytes=64)
            grouped_words = a_grouped[j][:].rearrange("p g b t -> p (g b t)").bitcast(F32).rearrange("p (g b h) -> p g b h", g=N_CHUNKS, h=2)
            chunks = slice(i * RUN, (i + 1) * RUN)
            copy(out=grouped_words[:, chunks, :, :], in_=a_banks[step][:].rearrange("p g h b -> p g b h"))

        def quantise_half(j, h):
            if h == 0:
                a_mx[j] = (
                    stage.tile([P, N_CHUNKS * P], U32, name="a_codes", tag="a_codes", align_bytes=64),
                    stage.tile([P, N_CHUNKS * P], U8, name="a_scales", tag="a_scales", align_bytes=64),
                )
            a_codes, a_scales = a_mx[j]
            chunks = slice(h * N_CHUNKS // 2, (h + 1) * N_CHUNKS // 2)
            words = slice(h * N_CHUNKS // 2 * P, (h + 1) * N_CHUNKS // 2 * P)
            nc.vector.quantize_mx(
                out=a_codes[:, words].bitcast(FP8X4),
                scales=a_scales[:, words],
                in_=a_grouped[j][:, chunks, :, :].rearrange("p g b t -> p (g b t)"),
            )

        def row_sum_of(j):
            row_sums[j] = small.tile([P, 1], F32, name="row_sum", tag="row_sum")
            nc.vector.tensor_reduce(out=row_sums[j][:], in_=abs_sums[j][:], axis=AXIS.X, op=ALU.add)

        def row_sum_but_last(j):
            early_sums[j] = small.tile([P, 1], F32, name="early_sum", tag="early_sum")
            nc.vector.tensor_reduce(out=early_sums[j][:], in_=abs_sums[j][:, 0 : SUMS - 2], axis=AXIS.X, op=ALU.add)

        def add_vector_sum(j):
            late_sums[j] = small.tile([P, 1], F32, name="late_sum", tag="late_sum")
            nc.vector.tensor_scalar(
                out=late_sums[j][:], in0=early_sums[j][:], scalar1=abs_sums[j][:, SUMS - 1 : SUMS], scalar2=None, op0=ALU.add
            )

        def add_scalar_sum(j):
            row_sums[j] = small.tile([P, 1], F32, name="row_sum", tag="row_sum")
            nc.vector.tensor_scalar(
                out=row_sums[j][:], in0=late_sums[j][:], scalar1=abs_sums[j][:, SUMS - 2 : SUMS - 1], scalar2=EPS, op0=ALU.add, op1=ALU.max
            )

        def invert_last(j):
            inv_sums[j] = small.tile([P, 1], F32, name="inv_sum", tag="inv_sum")
            nc.vector.reciprocal(out=inv_sums[j][:], in_=row_sums[j][:])

        def invert(j):
            inv_raws[j] = small.tile([P, 1], F32, name="inv_raw", tag="inv_raw")
            nc.vector.reciprocal(out=inv_raws[j][:], in_=row_sums[j][:])

        def clamp(j):
            inv_sums[j] = small.tile([P, 1], F32, name="inv_sum", tag="inv_sum")
            nc.vector.tensor_scalar(out=inv_sums[j][:], in0=inv_raws[j][:], scalar1=1.0 / EPS, scalar2=None, op0=ALU.min)

        def echo_matmuls(j):
            a_codes, a_scales = a_mx[j]
            if j < B_TILES - 2:
                echo_banks[j] = psum_t.tile([P, P], F32, name="echo_ps", tag="t")
            else:
                echo_banks[j] = psum_s.tile([P, P], F32, name="echo_ps", tag="s")
            for g in range(N_CHUNKS):
                cols = slice(g * P, (g + 1) * P)
                nc.tensor.matmul_mx(
                    out=echo_banks[j][:],
                    lhsT=e_codes[:, cols].bitcast(FP8X4),
                    lhsT_scale=e_scales[:, cols],
                    rhs=a_codes[:, cols].bitcast(FP8X4),
                    rhs_scale=a_scales[:, cols],
                    start=(g == 0),
                    stop=(g == N_CHUNKS - 1),
                )

        def echo_out(j, copy):
            echo = small.tile([P, P], F32, tag="echo")
            copy(out=echo[:], in_=echo_banks[j][:])
            echo_sq = small.tile([P, P], F32, tag="echo_sq")
            nc.scalar.activation(out=echo_sq[:], in_=echo_banks[j][:], func=ACT.Square)
            echoes[j] = (echo, echo_sq)

        def class_terms(j):
            d_banks[j] = psum_t.tile([P, L_PAD], F32, name="d_ps", tag="t")
            nc.tensor.matmul(out=d_banks[j][:], lhsT=ones[:], rhs=cls_sq[:], start=True, stop=False)

        def echo_terms(j):
            echo, echo_sq = echoes[j]
            nc.tensor.matmul(out=d_banks[j][:], lhsT=echo[:], rhs=cls_m2[:], start=False, stop=False)
            nc.tensor.matmul(out=d_banks[j][:], lhsT=echo_sq[:], rhs=ones[:, 0:L_PAD], start=False, stop=True)

        def distance_out(j):
            nc.scalar.activation(out=dist_sq[:, j, :], in_=d_banks[j][:, 0:L], func=ACT.Relu)

        def roots(tiles):
            nc.scalar.activation(out=dist[:, tiles, :], in_=dist_sq[:, tiles, :], func=ACT.Sqrt)
            nc.scalar.mul(result[:, tiles, :], dist[:, tiles, :], -1.0)

        def quantise_piece(step):
            j, i = divmod(step, STEPS_PER_TILE)
            if i == 0:
                a_mx[j] = (
                    stage.tile([P, N_CHUNKS * P], U32, name="a_codes", tag="a_codes", align_bytes=64),
                    stage.tile([P, N_CHUNKS * P], U8, name="a_scales", tag="a_scales", align_bytes=64),
                )
            a_codes, a_scales = a_mx[j]
            words = slice(i * RUN * P, (i + 1) * RUN * P)
            nc.vector.quantize_mx(
                out=a_codes[:, words].bitcast(FP8X4),
                scales=a_scales[:, words],
                in_=a_grouped[j][:, i * RUN : (i + 1) * RUN, :, :].rearrange("p g b t -> p (g b t)"),
            )

        for i in range(1 + PREPARE_AHEAD):
            prepare_next()

        cls_ps = psum_t.tile([P, P], BF16, tag="t")
        nc.tensor.transpose(cls_ps[:], cls_pad[:], ident_bf16[:])
        cls_t = consts.tile([P, L_PAD], F32)
        nc.vector.tensor_copy(out=cls_t[:], in_=cls_ps[:, 0:L_PAD])
        cls_m2 = consts.tile([P, L_PAD], F32)
        nc.vector.tensor_scalar(out=cls_m2[:], in0=cls_t[:], scalar1=-2.0, scalar2=None, op0=ALU.mult)
        cls_sq = consts.tile([P, L_PAD], F32)
        nc.vector.tensor_tensor(out=cls_sq[:], in0=cls_t[:], in1=cls_t[:], op=ALU.mult)

        for step in range(STEPS):
            summed = tile_ending_at(step - SUM_LAG)

            if step >= NORM_LAG:
                normalise(step - NORM_LAG, "gpsimd")

            if summed is not None:
                sum_last_magnitudes(summed)

            for j, c in units_of(step):
                similarities(j, c)
                if j == 0:
                    prepare_next()
            for j, c in units_of(step):
                cube(j, c)
            if step == STEPS - 1:
                sum_last_magnitudes(B_TILES - 1)

            if step >= SUM_LAG:
                sum_magnitudes(step - SUM_LAG)

            for group in groups_of(step):
                transpose_group(group)
            r = step - F_STEP
            if r == 0:
                f_raw = take_block(E_BLOCK + 1)
                f_grouped = new_grouped()
            if 0 <= r < F_PIECES[3][1]:
                transpose_probe_tile(f_raw, f_grouped, F_PIECES[3][1], r, nc.scalar.copy)

            if summed is not None:
                row_sum_of(summed)
            if step < STEPS - 1:
                for group in groups_of(step):
                    copy_group(group, nc.vector.tensor_copy)
            if summed is not None:
                invert(summed)
            if step >= QUANT_LAG and (step - QUANT_LAG + 1) % HALF_STEPS == 0:
                quantise_half(*divmod((step - QUANT_LAG) // HALF_STEPS, 2))
            if summed is not None:
                clamp(summed)

            if step == E_STEP:
                e_raw = take_block(E_BLOCK)
                e_grouped = stage.tile([P, N_CHUNKS, C, PACK], BF16, name="e_grouped", tag="a_grouped", align_bytes=64)
                for i in range(E_PIECES):
                    group_class_vectors(e_raw, e_grouped, i)
            if step == E_QUANT_STEP:
                nc.vector.quantize_mx(
                    out=e_codes[:].bitcast(FP8X4), scales=e_scales[:], in_=e_grouped[:].rearrange("p g c t -> p (g c t)")
                )
            if step == F_STEP + F_PIECES[3][1]:
                quantise_probes(f_grouped, 3)

            j = tile_ending_at(step - ECHO_LAG)
            if j is not None:
                echo_matmuls(j)
                echo_out(j, nc.scalar.copy)
            j = tile_ending_at(step - DIST_LAG)
            if j is not None:
                class_terms(j)
                echo_terms(j)
                distance_out(j)

        last = B_TILES - 1
        first_left = STEPS - GROUP_LAG
        normalise(STEPS - NORM_LAG, "gpsimd")
        sum_magnitudes(STEPS - 1)
        transpose_group(first_left)
        echo_matmuls(last - 2)
        transpose_group(first_left + 1)
        row_sum_but_last(last)
        copy_group(first_left - 2, nc.scalar.copy)
        add_vector_sum(last)
        echo_out(last - 2, nc.scalar.copy)
        class_terms(last - 2)
        echo_terms(last - 2)
        copy_group(first_left - 1, nc.scalar.copy)
        add_scalar_sum(last)
        copy_group(first_left, nc.scalar.copy)
        copy_group(first_left + 1, nc.scalar.copy)
        distance_out(last - 2)
        invert_last(last)
        quantise_piece(first_left - 2)
        for i in range(STEPS_PER_TILE):
            normalise(LAST_TILE_STEP + i, "vector")
        for i in range(STEPS_PER_TILE):
            transpose_group(LAST_TILE_STEP + i)
        copy_group(LAST_TILE_STEP, nc.scalar.copy)
        class_terms(last - 1)
        copy_group(LAST_TILE_STEP + 1, nc.scalar.copy)
        class_terms(last)
        quantise_piece(first_left - 1)
        quantise_piece(first_left)
        copy_group(LAST_TILE_STEP + 2, nc.scalar.copy)
        quantise_piece(first_left + 1)
        echo_matmuls(last - 1)
        quantise_piece(LAST_TILE_STEP)
        copy_group(LAST_TILE_STEP + 3, nc.scalar.copy)
        roots(slice(0, last - 1))
        quantise_piece(LAST_TILE_STEP + 1)
        quantise_piece(LAST_TILE_STEP + 2)
        quantise_piece(LAST_TILE_STEP + 3)
        echo_out(last - 1, nc.vector.tensor_copy)
        echo_matmuls(last)
        echo_out(last, nc.vector.tensor_copy)
        echo_terms(last - 1)
        echo_terms(last)
        distance_out(last - 1)
        distance_out(last)
        roots(slice(last - 1, B_TILES))
        nc.sync.dma_start(out=out.rearrange("(p j) l -> p j l", j=B_TILES), in_=result[:])
